import numpy as np
import ml_dtypes


def mxq(x, axis, fmt="e4m3"):
    dtype, down = {"e4m3": (ml_dtypes.float8_e4m3fn, 7), "e5m2": (ml_dtypes.float8_e5m2, 14)}[fmt]
    v = np.moveaxis(np.asarray(x, np.float32).astype(ml_dtypes.bfloat16).astype(np.float64), axis, -1)
    blocks = v.reshape(v.shape[:-1] + (-1, 32))
    amax = np.abs(blocks).max(-1, keepdims=True)
    byte = np.maximum(np.where(amax > 0, np.frexp(amax)[1] - 1 + 127, 0) - down, 1)
    scale = np.exp2(byte - 127.0)
    codes = (blocks / scale).astype(np.float32).astype(dtype).astype(np.float64)
    return np.moveaxis((codes * scale).reshape(v.shape), -1, axis)


WIDE = False


def mx_kscale(k):
    if not WIDE:
        return np.ones(k)
    levels = np.array([10, -10, 5, -5, 0])
    a = np.random.permutation(np.resize(levels, k // 512 * 4)).reshape(k // 512, 4)
    idx = np.arange(k)
    return np.exp2(a[idx // 512, idx % 128 // 32])


BF16 = ml_dtypes.bfloat16


def bf(x):
    return np.asarray(x, np.float32).astype(BF16)


def f64(x):
    return np.asarray(x).astype(np.float64)


B, L, S, T, Q, F, H, O = 4, 256, 32, 64, 1024, 1024, 1024, 768


def setup_inputs():
    s, u = mx_kscale(F), mx_kscale(F)
    return {"q": bf(np.random.standard_normal((B, L, H)) * 3.0),
            "src": bf(np.random.standard_normal((B, S, F)) * s),
            "trg": bf(np.random.standard_normal((B, T, F)) * u),
            "Ws": bf(np.random.standard_normal((F, H)) / np.sqrt(F) / s[:, None]),
            "b_s": bf(np.random.standard_normal(H) * 0.3),
            "Wt": bf(np.random.standard_normal((F, H)) / np.sqrt(F) / u[:, None]),
            "b_t": bf(np.random.standard_normal(H) * 0.3)}


def reference(q, src, trg, Ws, b_s, Wt, b_t):
    s_key = (mxq(f64(src), 2, "e4m3") @ mxq(f64(Ws), 0, "e4m3")) + f64(b_s)
    t_key = (mxq(f64(trg), 2, "e4m3") @ mxq(f64(Wt), 0, "e4m3")) + f64(b_t)
    rel_key = np.tanh(s_key[:, None, :, :] + t_key[:, :, None, :]).reshape(B, T * S, H)
    w = (mxq(f64(q), 2, "e4m3") @ mxq(rel_key, 2, "e4m3").transpose(0, 2, 1)) / np.sqrt(H)
    return w.reshape(B, L, T, S)

@@ -1,0 +1,251 @@
+from contextlib import ExitStack
+
+import concourse.mybir as mybir
+from concourse.masks import make_identity
+
+F32 = mybir.dt.float32
+BF16 = mybir.dt.bfloat16
+U32 = mybir.dt.uint32
+U8 = mybir.dt.uint8
+FP8X4 = mybir.dt.float8_e4m3fn_x4
+ADD = mybir.AluOpType.add
+TANH = mybir.ActivationFunctionType.Tanh
+
+B, L, S, T, F, H = 4, 256, 32, 64, 1024, 1024
+P = 128
+PACK = 4
+K_PASS = P * PACK
+PASSES = F // K_PASS
+T_CHUNK = 16
+N_COLS = T_CHUNK * S
+L_TILES = L // P
+SRC_TILES = B * S // P
+TOKEN_TILES = SRC_TILES + B * T // P
+
+FLOPS = 2 * (B * S + B * T) * F * H + 2 * B * L * T * S * H
+
+
+def quantise_rows(nc, psum_turn, stage, ident, rows, codes, scales):
+    words = rows.bitcast(F32)
+    turned = psum_turn.tile([P, PASSES * 2, P], F32)
+    for gu in range(PASSES * 2):
+        nc.tensor.transpose(turned[:, gu, :], words[:, gu * P : (gu + 1) * P], ident)
+    grouped = stage.tile([P, PASSES, P, PACK], BF16, align_bytes=64)
+    nc.scalar.copy(
+        out=grouped[:].bitcast(F32),
+        in_=turned[:].rearrange("p (g u) r -> p g r u", u=2),
+    )
+    nc.vector.quantize_mx(
+        out=codes.rearrange("p g r -> p (g r)").bitcast(FP8X4),
+        scales=scales.rearrange("p g r -> p (g r)"),
+        in_=grouped[:].rearrange("p g r j -> p (g r j)"),
+    )
+
+
+def tile_dynamicattention4_pa_kernel(tc, q, src, trg, Ws, b_s, Wt, b_t, out):
+    nc = tc.nc
+    with ExitStack() as ctx:
+        keep = ctx.enter_context(tc.tile_pool(name="keep", bufs=1))
+        stage = ctx.enter_context(tc.tile_pool(name="stage", bufs=3))
+        work = ctx.enter_context(tc.tile_pool(name="work", bufs=3))
+        psum_turn = ctx.enter_context(tc.psum_pool(name="psum_turn", bufs=2))
+        psum_keys = ctx.enter_context(tc.psum_pool(name="psum_keys", bufs=2))
+        psum_acc = ctx.enter_context(tc.psum_pool(name="psum_acc", bufs=2))
+
+        token_rows = keep.tile([P, TOKEN_TILES, F], BF16)
+        nc.sync.dma_start(out=token_rows[:, 0, :], in_=src.flatten_outer_dims())
+        nc.sync.dma_start(
+            out=token_rows[:, SRC_TILES:, :],
+            in_=trg.flatten_outer_dims().rearrange("(i p) f -> p i f", p=P),
+        )
+
+        weights = {"s": Ws, "t": Wt}
+        w_rows = {
+            name: keep.tile([P, PASSES, PACK, H], BF16, name="w_rows_" + name)
+            for name in weights
+        }
+        q_rows = keep.tile([P, B * L_TILES, H], BF16)
+
+        def load_weight_columns(gh):
+            cols = slice(gh * K_PASS, (gh + 1) * K_PASS)
+            for name in weights:
+                for g in range(PASSES):
+                    for u in range(2):
+                        first = g * K_PASS + u * 2 * P
+                        nc.sync.dma_start(
+                            out=w_rows[name][:, g, 2 * u : 2 * u + 2, cols],
+                            in_=weights[name][first : first + 2 * P, cols].rearrange(
+                                "(p e) c -> p e c", e=2
+                            ),
+                        )
+
+        def load_q(b):
+            nc.sync.dma_start(
+                out=q_rows[:, b * L_TILES : (b + 1) * L_TILES, :],
+                in_=q[b].rearrange("(i p) h -> p i h", p=P),
+            )
+
+        load_weight_columns(0)
+        load_q(0)
+        load_weight_columns(1)
+        for b in range(1, B):
+            load_q(b)
+
+        ident = keep.tile([P, P], F32)
+        make_identity(nc, ident[:])
+
+        bias_rows = keep.tile([P, 2 * P], BF16)
+        nc.vector.memset(bias_rows[:], 0.0)
+        bias_row_count = H // (2 * P)
+        nc.gpsimd.dma_start(
+            out=bias_rows[0:bias_row_count, :], in_=b_s.rearrange("(r c) -> r c", c=2 * P)
+        )
+        nc.gpsimd.dma_start(
+            out=bias_rows[bias_row_count : 2 * bias_row_count, :],
+            in_=b_t.rearrange("(r c) -> r c", c=2 * P),
+        )
+        turned = psum_turn.tile([P, PASSES * 2, P], F32)
+        nc.tensor.transpose(turned[:, 0, :], bias_rows[:].bitcast(F32), ident[:])
+        bias_cols = keep.tile([P, 2, PASSES * PACK], F32)
+        nc.vector.tensor_copy(
+            out=bias_cols[:].rearrange("p w c -> p (w c)"),
+            in_=turned[:, 0, 0 : 2 * bias_row_count].bitcast(BF16),
+        )
+        bias_sum = keep.tile([P, PASSES, PACK], F32)
+        nc.vector.tensor_tensor(
+            out=bias_sum[:].rearrange("p g j -> p (g j)"),
+            in0=bias_cols[:, 0, :],
+            in1=bias_cols[:, 1, :],
+            op=ADD,
+        )
+
+        token_codes = keep.tile([P, TOKEN_TILES, PASSES, P], U32, align_bytes=64)
+        token_scales = keep.tile([P, TOKEN_TILES, PASSES, P], U8, align_bytes=64)
+        for i in range(TOKEN_TILES):
+            quantise_rows(
+                nc, psum_turn, stage, ident[:],
+                token_rows[:, i, :], token_codes[:, i, :, :], token_scales[:, i, :, :],
+            )
+
+        w_codes = {
+            name: keep.tile([P, PASSES, H], U32, name="w_codes_" + name, align_bytes=64)
+            for name in weights
+        }
+        w_scales = {
+            name: keep.tile([P, PASSES, H], U8, name="w_scales_" + name, align_bytes=64)
+            for name in weights
+        }
+
+        def quantise_weight_columns(gh):
+            cols = slice(gh * K_PASS, (gh + 1) * K_PASS)
+            for name in weights:
+                for g in range(PASSES):
+                    w_grouped = stage.tile([P, K_PASS, PACK], BF16, align_bytes=64)
+                    for u in range(2):
+                        half = slice(u * 2 * P, (u + 1) * 2 * P)
+                        first = gh * K_PASS + u * 2 * P
+                        copy = nc.vector.tensor_copy if u == 0 else nc.scalar.copy
+                        copy(
+                            out=w_grouped[:, half, :].rearrange("p (e c) j -> p e c j", e=2),
+                            in_=w_rows[name][:, g, :, first : first + 2 * P].rearrange(
+                                "p j (c e) -> p e c j", e=2
+                            ),
+                        )
+                    nc.vector.quantize_mx(
+                        out=w_codes[name][:, g, cols].bitcast(FP8X4),
+                        scales=w_scales[name][:, g, cols],
+                        in_=w_grouped[:].rearrange("p c j -> p (c j)"),
+                    )
+
+        s_keys = keep.tile([P, PASSES, B * S, PACK], F32)
+        t_keys = keep.tile([P, PASSES, B * T, PACK], F32)
+
+        def project(gh):
+            for i in range(TOKEN_TILES):
+                name = "s" if i < SRC_TILES else "t"
+                key_bank = psum_keys.tile([P, PACK, P], F32)
+                for j in range(PACK):
+                    cols = slice(gh * K_PASS + j * P, gh * K_PASS + (j + 1) * P)
+                    for g in range(PASSES):
+                        nc.tensor.matmul_mx(
+                            out=key_bank[:, j, :],
+                            lhsT=w_codes[name][:, g, cols].bitcast(FP8X4),
+                            lhsT_scale=w_scales[name][:, g, cols],
+                            rhs=token_codes[:, i, g, :].bitcast(FP8X4),
+                            rhs_scale=token_scales[:, i, g, :],
+                            start=(g == 0),
+                            stop=(g == PASSES - 1),
+                        )
+                by_row = key_bank[:].rearrange("p j r -> p r j")
+                if i < SRC_TILES:
+                    nc.vector.tensor_copy(out=s_keys[:, gh, :, :], in_=by_row)
+                else:
+                    rows = slice((i - SRC_TILES) * P, (i - SRC_TILES + 1) * P)
+                    nc.vector.tensor_tensor(
+                        out=t_keys[:, gh, rows, :],
+                        in0=by_row,
+                        in1=bias_sum[:, gh, :].unsqueeze(1).to_broadcast([P, P, PACK]),
+                        op=ADD,
+                    )
+
+        for gh in range(PASSES):
+            quantise_weight_columns(gh)
+            project(gh)
+
+        q_codes = keep.tile([P, B * L_TILES, PASSES, P], U32, align_bytes=64)
+        q_scales = keep.tile([P, B * L_TILES, PASSES, P], U8, align_bytes=64)
+
+        def quantise_q(b):
+            for i in range(b * L_TILES, (b + 1) * L_TILES):
+                quantise_rows(
+                    nc, psum_turn, stage, ident[:],
+                    q_rows[:, i, :], q_codes[:, i, :, :], q_scales[:, i, :, :],
+                )
+
+        quantise_q(0)
+        for b in range(B):
+            if b + 1 < B:
+                quantise_q(b + 1)
+            out_b = out[b].rearrange("(i p) t s -> p i (t s)", p=P)
+            for c in range(T // T_CHUNK):
+                acc = [
+                    psum_acc.tile([P, N_COLS], F32, name="acc%d" % i) for i in range(L_TILES)
+                ]
+                for gh in range(PASSES):
+                    key_sum = work.tile([P, T_CHUNK, S, PACK], F32)
+                    first_t = b * T + c * T_CHUNK
+                    nc.vector.tensor_tensor(
+                        out=key_sum[:],
+                        in0=s_keys[:, gh, b * S : (b + 1) * S, :]
+                        .unsqueeze(1)
+                        .to_broadcast([P, T_CHUNK, S, PACK]),
+                        in1=t_keys[:, gh, first_t : first_t + T_CHUNK, :]
+                        .unsqueeze(2)
+                        .to_broadcast([P, T_CHUNK, S, PACK]),
+                        op=ADD,
+                    )
+                    rel = work.tile([P, N_COLS * PACK], BF16, align_bytes=64)
+                    nc.scalar.activation(
+                        out=rel[:], in_=key_sum[:].rearrange("p t s j -> p (t s j)"), func=TANH
+                    )
+                    rel_codes = work.tile([P, N_COLS], U32, align_bytes=64)
+                    rel_scales = work.tile([P, N_COLS], U8, align_bytes=64)
+                    nc.vector.quantize_mx(
+                        out=rel_codes[:].bitcast(FP8X4), scales=rel_scales[:], in_=rel[:]
+                    )
+                    for i in range(L_TILES):
+                        nc.tensor.matmul_mx(
+                            out=acc[i][:],
+                            lhsT=q_codes[:, b * L_TILES + i, gh, :].bitcast(FP8X4),
+                            lhsT_scale=q_scales[:, b * L_TILES + i, gh, :],
+                            rhs=rel_codes[:].bitcast(FP8X4),
+                            rhs_scale=rel_scales[:],
+                            start=(gh == 0),
+                            stop=(gh == PASSES - 1),
+                        )
+                scores = work.tile([P, L_TILES, N_COLS], F32)
+                for i in range(L_TILES):
+                    nc.scalar.mul(out=scores[:, i, :], in_=acc[i][:], mul=H ** -0.5)
+                nc.sync.dma_start(
+                    out=out_b[:, :, c * N_COLS : (c + 1) * N_COLS], in_=scores[:]
+                )

@@ -18,6 +18,7 @@ K_PASS = P * PACK
 PASSES = F // K_PASS
 T_CHUNK = 16
 N_COLS = T_CHUNK * S
+T_GPSIMD = 4
 L_TILES = L // P
 SRC_TILES = B * S // P
 TOKEN_TILES = SRC_TILES + B * T // P
@@ -46,18 +47,20 @@ def tile_dynamicattention4_pa_kernel(tc, q, src, trg, Ws, b_s, Wt, b_t, out):
     nc = tc.nc
     with ExitStack() as ctx:
         keep = ctx.enter_context(tc.tile_pool(name="keep", bufs=1))
-        stage = ctx.enter_context(tc.tile_pool(name="stage", bufs=3))
-        work = ctx.enter_context(tc.tile_pool(name="work", bufs=3))
+        stage = ctx.enter_context(tc.tile_pool(name="stage", bufs=4))
+        work = ctx.enter_context(tc.tile_pool(name="work", bufs=4))
         psum_turn = ctx.enter_context(tc.psum_pool(name="psum_turn", bufs=2))
-        psum_keys = ctx.enter_context(tc.psum_pool(name="psum_keys", bufs=2))
+        psum_src = ctx.enter_context(tc.psum_pool(name="psum_src", bufs=1))
         psum_acc = ctx.enter_context(tc.psum_pool(name="psum_acc", bufs=2))
 
         token_rows = keep.tile([P, TOKEN_TILES, F], BF16)
-        nc.sync.dma_start(out=token_rows[:, 0, :], in_=src.flatten_outer_dims())
-        nc.sync.dma_start(
-            out=token_rows[:, SRC_TILES:, :],
-            in_=trg.flatten_outer_dims().rearrange("(i p) f -> p i f", p=P),
-        )
+
+        def load_tokens():
+            nc.sync.dma_start(out=token_rows[:, 0, :], in_=src.flatten_outer_dims())
+            nc.sync.dma_start(
+                out=token_rows[:, SRC_TILES:, :],
+                in_=trg.flatten_outer_dims().rearrange("(i p) f -> p i f", p=P),
+            )
 
         weights = {"s": Ws, "t": Wt}
         w_rows = {
@@ -66,18 +69,17 @@ def tile_dynamicattention4_pa_kernel(tc, q, src, trg, Ws, b_s, Wt, b_t, out):
         }
         q_rows = keep.tile([P, B * L_TILES, H], BF16)
 
-        def load_weight_columns(gh):
+        def load_weight_columns(name, gh):
             cols = slice(gh * K_PASS, (gh + 1) * K_PASS)
-            for name in weights:
-                for g in range(PASSES):
-                    for u in range(2):
-                        first = g * K_PASS + u * 2 * P
-                        nc.sync.dma_start(
-                            out=w_rows[name][:, g, 2 * u : 2 * u + 2, cols],
-                            in_=weights[name][first : first + 2 * P, cols].rearrange(
-                                "(p e) c -> p e c", e=2
-                            ),
-                        )
+            for g in range(PASSES):
+                for u in range(2):
+                    first = g * K_PASS + u * 2 * P
+                    nc.sync.dma_start(
+                        out=w_rows[name][:, g, 2 * u : 2 * u + 2, cols],
+                        in_=weights[name][first : first + 2 * P, cols].rearrange(
+                            "(p e) c -> p e c", e=2
+                        ),
+                    )
 
         def load_q(b):
             nc.sync.dma_start(
@@ -85,22 +87,26 @@ def tile_dynamicattention4_pa_kernel(tc, q, src, trg, Ws, b_s, Wt, b_t, out):
                 in_=q[b].rearrange("(i p) h -> p i h", p=P),
             )
 
-        load_weight_columns(0)
+        load_weight_columns("t", 0)
+        load_tokens()
+        load_weight_columns("s", 0)
         load_q(0)
-        load_weight_columns(1)
+        load_weight_columns("t", 1)
+        load_weight_columns("s", 1)
         for b in range(1, B):
             load_q(b)
 
         ident = keep.tile([P, P], F32)
-        make_identity(nc, ident[:])
+        nc.vector.memset(ident[:], 0.0)
+        make_identity(nc, ident[:], nomemset=True)
 
         bias_rows = keep.tile([P, 2 * P], BF16)
         nc.vector.memset(bias_rows[:], 0.0)
         bias_row_count = H // (2 * P)
-        nc.gpsimd.dma_start(
+        nc.scalar.dma_start(
             out=bias_rows[0:bias_row_count, :], in_=b_s.rearrange("(r c) -> r c", c=2 * P)
         )
-        nc.gpsimd.dma_start(
+        nc.scalar.dma_start(
             out=bias_rows[bias_row_count : 2 * bias_row_count, :],
             in_=b_t.rearrange("(r c) -> r c", c=2 * P),
         )
@@ -121,11 +127,13 @@ def tile_dynamicattention4_pa_kernel(tc, q, src, trg, Ws, b_s, Wt, b_t, out):
 
         token_codes = keep.tile([P, TOKEN_TILES, PASSES, P], U32, align_bytes=64)
         token_scales = keep.tile([P, TOKEN_TILES, PASSES, P], U8, align_bytes=64)
-        for i in range(TOKEN_TILES):
-            quantise_rows(
-                nc, psum_turn, stage, ident[:],
-                token_rows[:, i, :], token_codes[:, i, :, :], token_scales[:, i, :, :],
-            )
+
+        def quantise_tokens():
+            for i in range(TOKEN_TILES):
+                quantise_rows(
+                    nc, psum_turn, stage, ident[:],
+                    token_rows[:, i, :], token_codes[:, i, :, :], token_scales[:, i, :, :],
+                )
 
         w_codes = {
             name: keep.tile([P, PASSES, H], U32, name="w_codes_" + name, align_bytes=64)
@@ -136,34 +144,39 @@ def tile_dynamicattention4_pa_kernel(tc, q, src, trg, Ws, b_s, Wt, b_t, out):
             for name in weights
         }
 
-        def quantise_weight_columns(gh):
+        def quantise_weight_columns(name, gh):
             cols = slice(gh * K_PASS, (gh + 1) * K_PASS)
-            for name in weights:
-                for g in range(PASSES):
-                    w_grouped = stage.tile([P, K_PASS, PACK], BF16, align_bytes=64)
-                    for u in range(2):
-                        half = slice(u * 2 * P, (u + 1) * 2 * P)
-                        first = gh * K_PASS + u * 2 * P
-                        copy = nc.vector.tensor_copy if u == 0 else nc.scalar.copy
-                        copy(
-                            out=w_grouped[:, half, :].rearrange("p (e c) j -> p e c j", e=2),
-                            in_=w_rows[name][:, g, :, first : first + 2 * P].rearrange(
-                                "p j (c e) -> p e c j", e=2
-                            ),
-                        )
-                    nc.vector.quantize_mx(
-                        out=w_codes[name][:, g, cols].bitcast(FP8X4),
-                        scales=w_scales[name][:, g, cols],
-                        in_=w_grouped[:].rearrange("p c j -> p (c j)"),
+            for g in range(PASSES):
+                w_grouped = stage.tile([P, K_PASS, PACK], BF16, align_bytes=64)
+                for u in range(2):
+                    half = slice(u * 2 * P, (u + 1) * 2 * P)
+                    first = gh * K_PASS + u * 2 * P
+                    copy = nc.vector.tensor_copy if u == 0 else nc.scalar.copy
+                    copy(
+                        out=w_grouped[:, half, :].rearrange("p (e c) j -> p e c j", e=2),
+                        in_=w_rows[name][:, g, :, first : first + 2 * P].rearrange(
+                            "p j (c e) -> p e c j", e=2
+                        ),
                     )
+                nc.vector.quantize_mx(
+                    out=w_codes[name][:, g, cols].bitcast(FP8X4),
+                    scales=w_scales[name][:, g, cols],
+                    in_=w_grouped[:].rearrange("p c j -> p (c j)"),
+                )
 
         s_keys = keep.tile([P, PASSES, B * S, PACK], F32)
         t_keys = keep.tile([P, PASSES, B * T, PACK], F32)
+        s_banks = [
+            psum_src.tile([P, PACK, P], F32, name="s_bank%d" % gh) for gh in range(PASSES)
+        ]
 
         def project(gh):
             for i in range(TOKEN_TILES):
                 name = "s" if i < SRC_TILES else "t"
-                key_bank = psum_keys.tile([P, PACK, P], F32)
+                if i < SRC_TILES:
+                    key_bank = s_banks[gh]
+                else:
+                    key_bank = psum_turn.tile([P, PACK, P], F32, tag="turned")
                 for j in range(PACK):
                     cols = slice(gh * K_PASS + j * P, gh * K_PASS + (j + 1) * P)
                     for g in range(PASSES):
@@ -188,9 +201,13 @@ def tile_dynamicattention4_pa_kernel(tc, q, src, trg, Ws, b_s, Wt, b_t, out):
                         op=ADD,
                     )
 
-        for gh in range(PASSES):
-            quantise_weight_columns(gh)
-            project(gh)
+        quantise_weight_columns("t", 0)
+        quantise_tokens()
+        quantise_weight_columns("s", 0)
+        project(0)
+        quantise_weight_columns("t", 1)
+        quantise_weight_columns("s", 1)
+        project(1)
 
         q_codes = keep.tile([P, B * L_TILES, PASSES, P], U32, align_bytes=64)
         q_scales = keep.tile([P, B * L_TILES, PASSES, P], U8, align_bytes=64)
@@ -214,14 +231,26 @@ def tile_dynamicattention4_pa_kernel(tc, q, src, trg, Ws, b_s, Wt, b_t, out):
                 for gh in range(PASSES):
                     key_sum = work.tile([P, T_CHUNK, S, PACK], F32)
                     first_t = b * T + c * T_CHUNK
+                    t_vector = T_CHUNK - T_GPSIMD
                     nc.vector.tensor_tensor(
-                        out=key_sum[:],
+                        out=key_sum[:, 0:t_vector, :, :],
+                        in0=s_banks[gh][:, :, b * S : (b + 1) * S]
+                        .rearrange("p j s -> p s j")
+                        .unsqueeze(1)
+                        .to_broadcast([P, t_vector, S, PACK]),
+                        in1=t_keys[:, gh, first_t : first_t + t_vector, :]
+                        .unsqueeze(2)
+                        .to_broadcast([P, t_vector, S, PACK]),
+                        op=ADD,
+                    )
+                    nc.gpsimd.tensor_tensor(
+                        out=key_sum[:, t_vector:, :, :],
                         in0=s_keys[:, gh, b * S : (b + 1) * S, :]
                         .unsqueeze(1)
-                        .to_broadcast([P, T_CHUNK, S, PACK]),
-                        in1=t_keys[:, gh, first_t : first_t + T_CHUNK, :]
+                        .to_broadcast([P, T_GPSIMD, S, PACK]),
+                        in1=t_keys[:, gh, first_t + t_vector : first_t + T_CHUNK, :]
                         .unsqueeze(2)
-                        .to_broadcast([P, T_CHUNK, S, PACK]),
+                        .to_broadcast([P, T_GPSIMD, S, PACK]),
                         op=ADD,
                     )
                     rel = work.tile([P, N_COLS * PACK], BF16, align_bytes=64)
@@ -244,8 +273,8 @@ def tile_dynamicattention4_pa_kernel(tc, q, src, trg, Ws, b_s, Wt, b_t, out):
                             stop=(gh == PASSES - 1),
                         )
                 scores = work.tile([P, L_TILES, N_COLS], F32)
-                for i in range(L_TILES):
-                    nc.scalar.mul(out=scores[:, i, :], in_=acc[i][:], mul=H ** -0.5)
+                nc.scalar.mul(out=scores[:, 0, :], in_=acc[0][:], mul=H ** -0.5)
+                nc.vector.tensor_scalar_mul(out=scores[:, 1, :], in0=acc[1][:], scalar1=H ** -0.5)
                 nc.sync.dma_start(
                     out=out_b[:, :, c * N_COLS : (c + 1) * N_COLS], in_=scores[:]
                 )

@@ -19,6 +19,7 @@ PASSES = F // K_PASS
 T_CHUNK = 16
 N_COLS = T_CHUNK * S
 T_GPSIMD = 4
+T_VECTOR = T_CHUNK - T_GPSIMD
 L_TILES = L // P
 SRC_TILES = B * S // P
 TOKEN_TILES = SRC_TILES + B * T // P
@@ -26,20 +27,12 @@ TOKEN_TILES = SRC_TILES + B * T // P
 FLOPS = 2 * (B * S + B * T) * F * H + 2 * B * L * T * S * H
 
 
-def quantise_rows(nc, psum_turn, stage, ident, rows, codes, scales):
+def turn_rows(nc, bank, ident, rows, grouped):
     words = rows.bitcast(F32)
-    turned = psum_turn.tile([P, PASSES * 2, P], F32)
     for gu in range(PASSES * 2):
-        nc.tensor.transpose(turned[:, gu, :], words[:, gu * P : (gu + 1) * P], ident)
-    grouped = stage.tile([P, PASSES, P, PACK], BF16, align_bytes=64)
+        nc.tensor.transpose(bank[:, gu, :], words[:, gu * P : (gu + 1) * P], ident)
     nc.scalar.copy(
-        out=grouped[:].bitcast(F32),
-        in_=turned[:].rearrange("p (g u) r -> p g r u", u=2),
-    )
-    nc.vector.quantize_mx(
-        out=codes.rearrange("p g r -> p (g r)").bitcast(FP8X4),
-        scales=scales.rearrange("p g r -> p (g r)"),
-        in_=grouped[:].rearrange("p g r j -> p (g r j)"),
+        out=grouped.bitcast(F32), in_=bank[:].rearrange("p (g u) r -> p g r u", u=2)
     )
 
 
@@ -52,16 +45,24 @@ def tile_dynamicattention4_pa_kernel(tc, q, src, trg, Ws, b_s, Wt, b_t, out):
         psum_turn = ctx.enter_context(tc.psum_pool(name="psum_turn", bufs=2))
         psum_src = ctx.enter_context(tc.psum_pool(name="psum_src", bufs=1))
         psum_acc = ctx.enter_context(tc.psum_pool(name="psum_acc", bufs=2))
+        ctx.enter_context(tc.manual_schedule())
+
+        ident = keep.tile([P, P], F32)
+        nc.vector.memset(ident[:], 0.0)
+        make_identity(nc, ident[:], nomemset=True)
+
+        bias_rows = keep.tile([P, 2 * P], BF16)
+        nc.vector.memset(bias_rows[:], 0.0)
+        bias_row_count = H // (2 * P)
+        nc.gpsimd.dma_start(
+            out=bias_rows[0:bias_row_count, :], in_=b_s.rearrange("(r c) -> r c", c=2 * P)
+        )
+        nc.gpsimd.dma_start(
+            out=bias_rows[bias_row_count : 2 * bias_row_count, :],
+            in_=b_t.rearrange("(r c) -> r c", c=2 * P),
+        )
 
         token_rows = keep.tile([P, TOKEN_TILES, F], BF16)
-
-        def load_tokens():
-            nc.sync.dma_start(out=token_rows[:, 0, :], in_=src.flatten_outer_dims())
-            nc.sync.dma_start(
-                out=token_rows[:, SRC_TILES:, :],
-                in_=trg.flatten_outer_dims().rearrange("(i p) f -> p i f", p=P),
-            )
-
         weights = {"s": Ws, "t": Wt}
         w_rows = {
             name: keep.tile([P, PASSES, PACK, H], BF16, name="w_rows_" + name)
@@ -81,59 +82,20 @@ def tile_dynamicattention4_pa_kernel(tc, q, src, trg, Ws, b_s, Wt, b_t, out):
                         ),
                     )
 
-        def load_q(b):
+        load_weight_columns("t", 0)
+        nc.sync.dma_start(out=token_rows[:, 0, :], in_=src.flatten_outer_dims())
+        nc.sync.dma_start(
+            out=token_rows[:, SRC_TILES:, :],
+            in_=trg.flatten_outer_dims().rearrange("(i p) f -> p i f", p=P),
+        )
+        load_weight_columns("s", 0)
+        load_weight_columns("t", 1)
+        load_weight_columns("s", 1)
+        for b in range(B):
             nc.sync.dma_start(
                 out=q_rows[:, b * L_TILES : (b + 1) * L_TILES, :],
                 in_=q[b].rearrange("(i p) h -> p i h", p=P),
             )
-
-        load_weight_columns("t", 0)
-        load_tokens()
-        load_weight_columns("s", 0)
-        load_q(0)
-        load_weight_columns("t", 1)
-        load_weight_columns("s", 1)
-        for b in range(1, B):
-            load_q(b)
-
-        ident = keep.tile([P, P], F32)
-        nc.vector.memset(ident[:], 0.0)
-        make_identity(nc, ident[:], nomemset=True)
-
-        bias_rows = keep.tile([P, 2 * P], BF16)
-        nc.vector.memset(bias_rows[:], 0.0)
-        bias_row_count = H // (2 * P)
-        nc.scalar.dma_start(
-            out=bias_rows[0:bias_row_count, :], in_=b_s.rearrange("(r c) -> r c", c=2 * P)
-        )
-        nc.scalar.dma_start(
-            out=bias_rows[bias_row_count : 2 * bias_row_count, :],
-            in_=b_t.rearrange("(r c) -> r c", c=2 * P),
-        )
-        turned = psum_turn.tile([P, PASSES * 2, P], F32)
-        nc.tensor.transpose(turned[:, 0, :], bias_rows[:].bitcast(F32), ident[:])
-        bias_cols = keep.tile([P, 2, PASSES * PACK], F32)
-        nc.vector.tensor_copy(
-            out=bias_cols[:].rearrange("p w c -> p (w c)"),
-            in_=turned[:, 0, 0 : 2 * bias_row_count].bitcast(BF16),
-        )
-        bias_sum = keep.tile([P, PASSES, PACK], F32)
-        nc.vector.tensor_tensor(
-            out=bias_sum[:].rearrange("p g j -> p (g j)"),
-            in0=bias_cols[:, 0, :],
-            in1=bias_cols[:, 1, :],
-            op=ADD,
-        )
-
-        token_codes = keep.tile([P, TOKEN_TILES, PASSES, P], U32, align_bytes=64)
-        token_scales = keep.tile([P, TOKEN_TILES, PASSES, P], U8, align_bytes=64)
-
-        def quantise_tokens():
-            for i in range(TOKEN_TILES):
-                quantise_rows(
-                    nc, psum_turn, stage, ident[:],
-                    token_rows[:, i, :], token_codes[:, i, :, :], token_scales[:, i, :, :],
-                )
 
         w_codes = {
             name: keep.tile([P, PASSES, H], U32, name="w_codes_" + name, align_bytes=64)
@@ -143,26 +105,63 @@ def tile_dynamicattention4_pa_kernel(tc, q, src, trg, Ws, b_s, Wt, b_t, out):
             name: keep.tile([P, PASSES, H], U8, name="w_scales_" + name, align_bytes=64)
             for name in weights
         }
+        w_grouped = {}
 
-        def quantise_weight_columns(name, gh):
-            cols = slice(gh * K_PASS, (gh + 1) * K_PASS)
+        def regroup_weight_columns(name, gh):
             for g in range(PASSES):
-                w_grouped = stage.tile([P, K_PASS, PACK], BF16, align_bytes=64)
+                grouped = stage.tile([P, K_PASS, PACK], BF16, align_bytes=64, tag="w_grouped")
                 for u in range(2):
                     half = slice(u * 2 * P, (u + 1) * 2 * P)
                     first = gh * K_PASS + u * 2 * P
                     copy = nc.vector.tensor_copy if u == 0 else nc.scalar.copy
                     copy(
-                        out=w_grouped[:, half, :].rearrange("p (e c) j -> p e c j", e=2),
+                        out=grouped[:, half, :].rearrange("p (e c) j -> p e c j", e=2),
                         in_=w_rows[name][:, g, :, first : first + 2 * P].rearrange(
                             "p j (c e) -> p e c j", e=2
                         ),
                     )
+                w_grouped[(name, gh, g)] = grouped
+
+        def quantise_weight_columns(name, gh):
+            cols = slice(gh * K_PASS, (gh + 1) * K_PASS)
+            for g in range(PASSES):
                 nc.vector.quantize_mx(
                     out=w_codes[name][:, g, cols].bitcast(FP8X4),
                     scales=w_scales[name][:, g, cols],
-                    in_=w_grouped[:].rearrange("p c j -> p (c j)"),
+                    in_=w_grouped[(name, gh, g)][:].rearrange("p c j -> p (c j)"),
                 )
+
+        token_codes = keep.tile([P, TOKEN_TILES, PASSES, P], U32, align_bytes=64)
+        token_scales = keep.tile([P, TOKEN_TILES, PASSES, P], U8, align_bytes=64)
+        token_grouped = keep.tile([P, TOKEN_TILES, PASSES, P, PACK], BF16, align_bytes=64)
+
+        def quantise_tokens():
+            for i in range(TOKEN_TILES):
+                bank = psum_turn.tile([P, PASSES * 2, P], F32, tag="turned")
+                turn_rows(nc, bank, ident[:], token_rows[:, i, :], token_grouped[:, i])
+            for i in range(TOKEN_TILES):
+                nc.vector.quantize_mx(
+                    out=token_codes[:, i].rearrange("p g r -> p (g r)").bitcast(FP8X4),
+                    scales=token_scales[:, i].rearrange("p g r -> p (g r)"),
+                    in_=token_grouped[:, i].rearrange("p g r j -> p (g r j)"),
+                )
+
+        bias_sum = keep.tile([P, PASSES, PACK], F32)
+
+        def turn_biases():
+            bank = psum_turn.tile([P, PASSES * 2, P], F32, tag="turned")
+            nc.tensor.transpose(bank[:, 0, :], bias_rows[:].bitcast(F32), ident[:])
+            bias_cols = keep.tile([P, 2, PASSES * PACK], F32)
+            nc.vector.tensor_copy(
+                out=bias_cols[:].rearrange("p w c -> p (w c)"),
+                in_=bank[:, 0, 0 : 2 * bias_row_count].bitcast(BF16),
+            )
+            nc.vector.tensor_tensor(
+                out=bias_sum[:].rearrange("p g j -> p (g j)"),
+                in0=bias_cols[:, 0, :],
+                in1=bias_cols[:, 1, :],
+                op=ADD,
+            )
 
         s_keys = keep.tile([P, PASSES, B * S, PACK], F32)
         t_keys = keep.tile([P, PASSES, B * T, PACK], F32)
@@ -171,7 +170,7 @@ def tile_dynamicattention4_pa_kernel(tc, q, src, trg, Ws, b_s, Wt, b_t, out):
         ]
 
         def project(gh):
-            for i in range(TOKEN_TILES):
+            for i in list(range(SRC_TILES, TOKEN_TILES)) + list(range(SRC_TILES)):
                 name = "s" if i < SRC_TILES else "t"
                 if i < SRC_TILES:
                     key_bank = s_banks[gh]
@@ -201,80 +200,132 @@ def tile_dynamicattention4_pa_kernel(tc, q, src, trg, Ws, b_s, Wt, b_t, out):
                         op=ADD,
                     )
 
+        q_codes = keep.tile([P, B * L_TILES, PASSES, P], U32, align_bytes=64)
+        q_scales = keep.tile([P, B * L_TILES, PASSES, P], U8, align_bytes=64)
+        q_grouped = keep.tile([P, B * L_TILES, PASSES, P, PACK], BF16, align_bytes=64)
+
+        def turn_q(b):
+            for i in range(L_TILES):
+                bank = psum_acc.tile([P, PASSES * 2, P], F32, tag="acc%d" % i)
+                tile_index = b * L_TILES + i
+                turn_rows(nc, bank, ident[:], q_rows[:, tile_index, :], q_grouped[:, tile_index])
+
+        def quantise_q(b):
+            tiles = slice(b * L_TILES, (b + 1) * L_TILES)
+            nc.vector.quantize_mx(
+                out=q_codes[:, tiles].rearrange("p i g r -> p (i g r)").bitcast(FP8X4),
+                scales=q_scales[:, tiles].rearrange("p i g r -> p (i g r)"),
+                in_=q_grouped[:, tiles].rearrange("p i g r j -> p (i g r j)"),
+            )
+
+        units = [(b, c, gh) for b in range(B) for c in range(T // T_CHUNK) for gh in range(PASSES)]
+        key_sums = {}
+        rels = {}
+        accs = {}
+
+        def add_keys(n):
+            b, c, gh = units[n]
+            src_rows = slice(b * S, (b + 1) * S)
+            first_t = b * T + c * T_CHUNK
+            sum_v = work.tile([P, T_VECTOR, S, PACK], F32)
+            nc.vector.tensor_tensor(
+                out=sum_v[:],
+                in0=s_banks[gh][:, :, src_rows]
+                .rearrange("p j s -> p s j")
+                .unsqueeze(1)
+                .to_broadcast([P, T_VECTOR, S, PACK]),
+                in1=t_keys[:, gh, first_t : first_t + T_VECTOR, :]
+                .unsqueeze(2)
+                .to_broadcast([P, T_VECTOR, S, PACK]),
+                op=ADD,
+            )
+            sum_g = work.tile([P, T_GPSIMD, S, PACK], F32)
+            nc.gpsimd.tensor_tensor(
+                out=sum_g[:],
+                in0=s_keys[:, gh, src_rows, :].unsqueeze(1).to_broadcast([P, T_GPSIMD, S, PACK]),
+                in1=t_keys[:, gh, first_t + T_VECTOR : first_t + T_CHUNK, :]
+                .unsqueeze(2)
+                .to_broadcast([P, T_GPSIMD, S, PACK]),
+                op=ADD,
+            )
+            key_sums[n] = (sum_v, sum_g)
+
+        def take_tanh(n):
+            sum_v, sum_g = key_sums[n]
+            rel = work.tile([P, N_COLS * PACK], BF16, align_bytes=64)
+            split = T_VECTOR * S * PACK
+            nc.scalar.activation(
+                out=rel[:, split:], in_=sum_g[:].rearrange("p t s j -> p (t s j)"), func=TANH
+            )
+            nc.scalar.activation(
+                out=rel[:, :split], in_=sum_v[:].rearrange("p t s j -> p (t s j)"), func=TANH
+            )
+            rels[n] = rel
+
+        def multiply(n):
+            b, c, gh = units[n]
+            rel_codes = work.tile([P, N_COLS], U32, align_bytes=64)
+            rel_scales = work.tile([P, N_COLS], U8, align_bytes=64)
+            nc.vector.quantize_mx(
+                out=rel_codes[:].bitcast(FP8X4), scales=rel_scales[:], in_=rels[n][:]
+            )
+            if gh == 0:
+                accs[(b, c)] = [
+                    psum_acc.tile([P, N_COLS], F32, name="acc%d" % i) for i in range(L_TILES)
+                ]
+            for i in range(L_TILES):
+                nc.tensor.matmul_mx(
+                    out=accs[(b, c)][i][:],
+                    lhsT=q_codes[:, b * L_TILES + i, gh, :].bitcast(FP8X4),
+                    lhsT_scale=q_scales[:, b * L_TILES + i, gh, :],
+                    rhs=rel_codes[:].bitcast(FP8X4),
+                    rhs_scale=rel_scales[:],
+                    start=(gh == 0),
+                    stop=(gh == PASSES - 1),
+                )
+
+        def store_scores(n):
+            b, c, gh = units[n]
+            acc = accs[(b, c)]
+            scores = work.tile([P, L_TILES, N_COLS], F32)
+            nc.scalar.mul(out=scores[:, 0, :], in_=acc[0][:], mul=H ** -0.5)
+            nc.vector.tensor_scalar_mul(out=scores[:, 1, :], in0=acc[1][:], scalar1=H ** -0.5)
+            nc.sync.dma_start(
+                out=out[b].rearrange("(i p) t s -> p i (t s)", p=P)[
+                    :, :, c * N_COLS : (c + 1) * N_COLS
+                ],
+                in_=scores[:],
+            )
+
+        regroup_weight_columns("t", 0)
         quantise_weight_columns("t", 0)
         quantise_tokens()
+        regroup_weight_columns("s", 0)
         quantise_weight_columns("s", 0)
+        turn_biases()
         project(0)
+        add_keys(0)
+        regroup_weight_columns("t", 1)
+        regroup_weight_columns("s", 1)
+        take_tanh(0)
+        turn_q(0)
+        turn_q(1)
         quantise_weight_columns("t", 1)
         quantise_weight_columns("s", 1)
         project(1)
-
-        q_codes = keep.tile([P, B * L_TILES, PASSES, P], U32, align_bytes=64)
-        q_scales = keep.tile([P, B * L_TILES, PASSES, P], U8, align_bytes=64)
-
-        def quantise_q(b):
-            for i in range(b * L_TILES, (b + 1) * L_TILES):
-                quantise_rows(
-                    nc, psum_turn, stage, ident[:],
-                    q_rows[:, i, :], q_codes[:, i, :, :], q_scales[:, i, :, :],
-                )
-
+        turn_q(2)
+        turn_q(3)
         quantise_q(0)
-        for b in range(B):
-            if b + 1 < B:
-                quantise_q(b + 1)
-            out_b = out[b].rearrange("(i p) t s -> p i (t s)", p=P)
-            for c in range(T // T_CHUNK):
-                acc = [
-                    psum_acc.tile([P, N_COLS], F32, name="acc%d" % i) for i in range(L_TILES)
-                ]
-                for gh in range(PASSES):
-                    key_sum = work.tile([P, T_CHUNK, S, PACK], F32)
-                    first_t = b * T + c * T_CHUNK
-                    t_vector = T_CHUNK - T_GPSIMD
-                    nc.vector.tensor_tensor(
-                        out=key_sum[:, 0:t_vector, :, :],
-                        in0=s_banks[gh][:, :, b * S : (b + 1) * S]
-                        .rearrange("p j s -> p s j")
-                        .unsqueeze(1)
-                        .to_broadcast([P, t_vector, S, PACK]),
-                        in1=t_keys[:, gh, first_t : first_t + t_vector, :]
-                        .unsqueeze(2)
-                        .to_broadcast([P, t_vector, S, PACK]),
-                        op=ADD,
-                    )
-                    nc.gpsimd.tensor_tensor(
-                        out=key_sum[:, t_vector:, :, :],
-                        in0=s_keys[:, gh, b * S : (b + 1) * S, :]
-                        .unsqueeze(1)
-                        .to_broadcast([P, T_GPSIMD, S, PACK]),
-                        in1=t_keys[:, gh, first_t + t_vector : first_t + T_CHUNK, :]
-                        .unsqueeze(2)
-                        .to_broadcast([P, T_GPSIMD, S, PACK]),
-                        op=ADD,
-                    )
-                    rel = work.tile([P, N_COLS * PACK], BF16, align_bytes=64)
-                    nc.scalar.activation(
-                        out=rel[:], in_=key_sum[:].rearrange("p t s j -> p (t s j)"), func=TANH
-                    )
-                    rel_codes = work.tile([P, N_COLS], U32, align_bytes=64)
-                    rel_scales = work.tile([P, N_COLS], U8, align_bytes=64)
-                    nc.vector.quantize_mx(
-                        out=rel_codes[:].bitcast(FP8X4), scales=rel_scales[:], in_=rel[:]
-                    )
-                    for i in range(L_TILES):
-                        nc.tensor.matmul_mx(
-                            out=acc[i][:],
-                            lhsT=q_codes[:, b * L_TILES + i, gh, :].bitcast(FP8X4),
-                            lhsT_scale=q_scales[:, b * L_TILES + i, gh, :],
-                            rhs=rel_codes[:].bitcast(FP8X4),
-                            rhs_scale=rel_scales[:],
-                            start=(gh == 0),
-                            stop=(gh == PASSES - 1),
-                        )
-                scores = work.tile([P, L_TILES, N_COLS], F32)
-                nc.scalar.mul(out=scores[:, 0, :], in_=acc[0][:], mul=H ** -0.5)
-                nc.vector.tensor_scalar_mul(out=scores[:, 1, :], in0=acc[1][:], scalar1=H ** -0.5)
-                nc.sync.dma_start(
-                    out=out_b[:, :, c * N_COLS : (c + 1) * N_COLS], in_=scores[:]
-                )
+
+        units_per_batch = len(units) // B
+        for n in range(1, len(units) + 3):
+            if n < len(units):
+                add_keys(n)
+            if 0 <= n - 2 < len(units):
+                multiply(n - 2)
+            if 0 <= n - 3 and units[n - 3][2] == PASSES - 1:
+                store_scores(n - 3)
+            if n < len(units):
+                take_tanh(n)
+                if n % units_per_batch == 1 and n // units_per_batch + 1 < B:
+                    quantise_q(n // units_per_batch + 1)

@@ -62,49 +62,49 @@ def tile_dynamicattention4_pa_kernel(tc, q, src, trg, Ws, b_s, Wt, b_t, out):
             in_=b_t.rearrange("(r c) -> r c", c=2 * P),
         )
 
-        token_rows = keep.tile([P, TOKEN_TILES, F], BF16)
         weights = {"s": Ws, "t": Wt}
-        w_rows = {
-            name: keep.tile([P, PASSES, PACK, H], BF16, name="w_rows_" + name)
-            for name in weights
-        }
-        q_rows = keep.tile([P, B * L_TILES, H], BF16)
+        w_rows = {}
 
         def load_weight_columns(name, gh):
             cols = slice(gh * K_PASS, (gh + 1) * K_PASS)
             for g in range(PASSES):
+                rows = keep.tile([P, PACK, K_PASS], BF16, name="w_rows_%s%d%d" % (name, gh, g))
                 for u in range(2):
                     first = g * K_PASS + u * 2 * P
                     nc.sync.dma_start(
-                        out=w_rows[name][:, g, 2 * u : 2 * u + 2, cols],
+                        out=rows[:, 2 * u : 2 * u + 2, :],
                         in_=weights[name][first : first + 2 * P, cols].rearrange(
                             "(p e) c -> p e c", e=2
                         ),
                     )
+                w_rows[(name, gh, g)] = rows
 
         load_weight_columns("t", 0)
-        nc.sync.dma_start(out=token_rows[:, 0, :], in_=src.flatten_outer_dims())
-        nc.sync.dma_start(
-            out=token_rows[:, SRC_TILES:, :],
-            in_=trg.flatten_outer_dims().rearrange("(i p) f -> p i f", p=P),
-        )
+        tokens = [src.flatten_outer_dims()] + [
+            trg.flatten_outer_dims()[i * P : (i + 1) * P, :] for i in range(TOKEN_TILES - SRC_TILES)
+        ]
+        token_rows = [
+            keep.tile([P, F], BF16, name="token_rows%d" % i) for i in range(TOKEN_TILES)
+        ]
+        for i in range(TOKEN_TILES):
+            nc.sync.dma_start(out=token_rows[i][:], in_=tokens[i])
         load_weight_columns("s", 0)
         load_weight_columns("t", 1)
         load_weight_columns("s", 1)
+        q_rows = [keep.tile([P, L_TILES, H], BF16, name="q_rows%d" % b) for b in range(B)]
         for b in range(B):
-            nc.sync.dma_start(
-                out=q_rows[:, b * L_TILES : (b + 1) * L_TILES, :],
-                in_=q[b].rearrange("(i p) h -> p i h", p=P),
-            )
+            nc.sync.dma_start(out=q_rows[b][:], in_=q[b].rearrange("(i p) h -> p i h", p=P))
 
-        w_codes = {
-            name: keep.tile([P, PASSES, H], U32, name="w_codes_" + name, align_bytes=64)
-            for name in weights
-        }
-        w_scales = {
-            name: keep.tile([P, PASSES, H], U8, name="w_scales_" + name, align_bytes=64)
-            for name in weights
-        }
+        w_codes = {}
+        w_scales = {}
+        for name in weights:
+            for gh in range(PASSES):
+                w_codes[(name, gh)] = keep.tile(
+                    [P, PASSES, K_PASS], U32, name="w_codes_%s%d" % (name, gh), align_bytes=64
+                )
+                w_scales[(name, gh)] = keep.tile(
+                    [P, PASSES, K_PASS], U8, name="w_scales_%s%d" % (name, gh), align_bytes=64
+                )
         w_grouped = {}
 
         def regroup_weight_columns(name, gh):
@@ -112,22 +112,20 @@ def tile_dynamicattention4_pa_kernel(tc, q, src, trg, Ws, b_s, Wt, b_t, out):
                 grouped = stage.tile([P, K_PASS, PACK], BF16, align_bytes=64, tag="w_grouped")
                 for u in range(2):
                     half = slice(u * 2 * P, (u + 1) * 2 * P)
-                    first = gh * K_PASS + u * 2 * P
                     copy = nc.vector.tensor_copy if u == 0 else nc.scalar.copy
                     copy(
                         out=grouped[:, half, :].rearrange("p (e c) j -> p e c j", e=2),
-                        in_=w_rows[name][:, g, :, first : first + 2 * P].rearrange(
+                        in_=w_rows[(name, gh, g)][:, :, half].rearrange(
                             "p j (c e) -> p e c j", e=2
                         ),
                     )
                 w_grouped[(name, gh, g)] = grouped
 
         def quantise_weight_columns(name, gh):
-            cols = slice(gh * K_PASS, (gh + 1) * K_PASS)
             for g in range(PASSES):
                 nc.vector.quantize_mx(
-                    out=w_codes[name][:, g, cols].bitcast(FP8X4),
-                    scales=w_scales[name][:, g, cols],
+                    out=w_codes[(name, gh)][:, g, :].bitcast(FP8X4),
+                    scales=w_scales[(name, gh)][:, g, :],
                     in_=w_grouped[(name, gh, g)][:].rearrange("p c j -> p (c j)"),
                 )
 
@@ -138,7 +136,7 @@ def tile_dynamicattention4_pa_kernel(tc, q, src, trg, Ws, b_s, Wt, b_t, out):
         def quantise_tokens():
             for i in range(TOKEN_TILES):
                 bank = psum_turn.tile([P, PASSES * 2, P], F32, tag="turned")
-                turn_rows(nc, bank, ident[:], token_rows[:, i, :], token_grouped[:, i])
+                turn_rows(nc, bank, ident[:], token_rows[i][:], token_grouped[:, i])
             for i in range(TOKEN_TILES):
                 nc.vector.quantize_mx(
                     out=token_codes[:, i].rearrange("p g r -> p (g r)").bitcast(FP8X4),
@@ -177,12 +175,12 @@ def tile_dynamicattention4_pa_kernel(tc, q, src, trg, Ws, b_s, Wt, b_t, out):
                 else:
                     key_bank = psum_turn.tile([P, PACK, P], F32, tag="turned")
                 for j in range(PACK):
-                    cols = slice(gh * K_PASS + j * P, gh * K_PASS + (j + 1) * P)
+                    cols = slice(j * P, (j + 1) * P)
                     for g in range(PASSES):
                         nc.tensor.matmul_mx(
                             out=key_bank[:, j, :],
-                            lhsT=w_codes[name][:, g, cols].bitcast(FP8X4),
-                            lhsT_scale=w_scales[name][:, g, cols],
+                            lhsT=w_codes[(name, gh)][:, g, cols].bitcast(FP8X4),
+                            lhsT_scale=w_scales[(name, gh)][:, g, cols],
                             rhs=token_codes[:, i, g, :].bitcast(FP8X4),
                             rhs_scale=token_scales[:, i, g, :],
                             start=(g == 0),
@@ -208,7 +206,7 @@ def tile_dynamicattention4_pa_kernel(tc, q, src, trg, Ws, b_s, Wt, b_t, out):
             for i in range(L_TILES):
                 bank = psum_acc.tile([P, PASSES * 2, P], F32, tag="acc%d" % i)
                 tile_index = b * L_TILES + i
-                turn_rows(nc, bank, ident[:], q_rows[:, tile_index, :], q_grouped[:, tile_index])
+                turn_rows(nc, bank, ident[:], q_rows[b][:, i, :], q_grouped[:, tile_index])
 
         def quantise_q(b):
             tiles = slice(b * L_TILES, (b + 1) * L_TILES)

@@ -18,7 +18,7 @@ K_PASS = P * PACK
 PASSES = F // K_PASS
 T_CHUNK = 16
 N_COLS = T_CHUNK * S
-T_GPSIMD = 4
+T_GPSIMD = 5
 T_VECTOR = T_CHUNK - T_GPSIMD
 L_TILES = L // P
 SRC_TILES = B * S // P

@@ -27,21 +27,22 @@ TOKEN_TILES = SRC_TILES + B * T // P
 FLOPS = 2 * (B * S + B * T) * F * H + 2 * B * L * T * S * H
 
 
-def turn_rows(nc, bank, ident, rows, grouped):
+def turn_rows(nc, bank, ident, rows):
     words = rows.bitcast(F32)
     for gu in range(PASSES * 2):
         nc.tensor.transpose(bank[:, gu, :], words[:, gu * P : (gu + 1) * P], ident)
-    nc.scalar.copy(
-        out=grouped.bitcast(F32), in_=bank[:].rearrange("p (g u) r -> p g r u", u=2)
-    )
+
+
+def group_rows(copy, bank, grouped):
+    copy(out=grouped.bitcast(F32), in_=bank[:].rearrange("p (g u) r -> p g r u", u=2))
 
 
 def tile_dynamicattention4_pa_kernel(tc, q, src, trg, Ws, b_s, Wt, b_t, out):
     nc = tc.nc
     with ExitStack() as ctx:
         keep = ctx.enter_context(tc.tile_pool(name="keep", bufs=1))
-        stage = ctx.enter_context(tc.tile_pool(name="stage", bufs=4))
-        work = ctx.enter_context(tc.tile_pool(name="work", bufs=4))
+        stage = ctx.enter_context(tc.tile_pool(name="stage", bufs=6))
+        work = ctx.enter_context(tc.tile_pool(name="work", bufs=3))
         psum_turn = ctx.enter_context(tc.psum_pool(name="psum_turn", bufs=2))
         psum_src = ctx.enter_context(tc.psum_pool(name="psum_src", bufs=1))
         psum_acc = ctx.enter_context(tc.psum_pool(name="psum_acc", bufs=2))
@@ -107,42 +108,46 @@ def tile_dynamicattention4_pa_kernel(tc, q, src, trg, Ws, b_s, Wt, b_t, out):
                 )
         w_grouped = {}
 
-        def regroup_weight_columns(name, gh):
-            for g in range(PASSES):
-                grouped = stage.tile([P, K_PASS, PACK], BF16, align_bytes=64, tag="w_grouped")
-                for u in range(2):
-                    half = slice(u * 2 * P, (u + 1) * 2 * P)
-                    copy = nc.vector.tensor_copy if u == 0 else nc.scalar.copy
-                    copy(
-                        out=grouped[:, half, :].rearrange("p (e c) j -> p e c j", e=2),
-                        in_=w_rows[(name, gh, g)][:, :, half].rearrange(
-                            "p j (c e) -> p e c j", e=2
-                        ),
-                    )
-                w_grouped[(name, gh, g)] = grouped
-
-        def quantise_weight_columns(name, gh):
-            for g in range(PASSES):
-                nc.vector.quantize_mx(
-                    out=w_codes[(name, gh)][:, g, :].bitcast(FP8X4),
-                    scales=w_scales[(name, gh)][:, g, :],
-                    in_=w_grouped[(name, gh, g)][:].rearrange("p c j -> p (c j)"),
+        def regroup(copy, u, name, gh, g):
+            key = (name, gh, g)
+            if key not in w_grouped:
+                w_grouped[key] = stage.tile(
+                    [P, K_PASS, PACK], BF16, align_bytes=64, tag="grouped", name="w_grouped"
                 )
+            half = slice(u * 2 * P, (u + 1) * 2 * P)
+            copy(
+                out=w_grouped[key][:, half, :].rearrange("p (e c) j -> p e c j", e=2),
+                in_=w_rows[key][:, :, half].rearrange("p j (c e) -> p e c j", e=2),
+            )
+
+        def regroup_v(name, gh, g):
+            regroup(nc.vector.tensor_copy, 0, name, gh, g)
+
+        def regroup_s(name, gh, g):
+            regroup(nc.scalar.copy, 1, name, gh, g)
+
+        def quantise_weight(name, gh, g):
+            nc.vector.quantize_mx(
+                out=w_codes[(name, gh)][:, g, :].bitcast(FP8X4),
+                scales=w_scales[(name, gh)][:, g, :],
+                in_=w_grouped[(name, gh, g)][:].rearrange("p c j -> p (c j)"),
+            )
 
         token_codes = keep.tile([P, TOKEN_TILES, PASSES, P], U32, align_bytes=64)
         token_scales = keep.tile([P, TOKEN_TILES, PASSES, P], U8, align_bytes=64)
         token_grouped = keep.tile([P, TOKEN_TILES, PASSES, P, PACK], BF16, align_bytes=64)
 
-        def quantise_tokens():
-            for i in range(TOKEN_TILES):
-                bank = psum_turn.tile([P, PASSES * 2, P], F32, tag="turned")
-                turn_rows(nc, bank, ident[:], token_rows[i][:], token_grouped[:, i])
-            for i in range(TOKEN_TILES):
-                nc.vector.quantize_mx(
-                    out=token_codes[:, i].rearrange("p g r -> p (g r)").bitcast(FP8X4),
-                    scales=token_scales[:, i].rearrange("p g r -> p (g r)"),
-                    in_=token_grouped[:, i].rearrange("p g r j -> p (g r j)"),
-                )
+        def turn_token(i):
+            bank = psum_turn.tile([P, PASSES * 2, P], F32, tag="turned")
+            turn_rows(nc, bank, ident[:], token_rows[i][:])
+            group_rows(nc.scalar.copy, bank, token_grouped[:, i])
+
+        def quantise_token(i):
+            nc.vector.quantize_mx(
+                out=token_codes[:, i].rearrange("p g r -> p (g r)").bitcast(FP8X4),
+                scales=token_scales[:, i].rearrange("p g r -> p (g r)"),
+                in_=token_grouped[:, i].rearrange("p g r j -> p (g r j)"),
+            )
 
         bias_sum = keep.tile([P, PASSES, PACK], F32)
 
@@ -167,56 +172,71 @@ def tile_dynamicattention4_pa_kernel(tc, q, src, trg, Ws, b_s, Wt, b_t, out):
             psum_src.tile([P, PACK, P], F32, name="s_bank%d" % gh) for gh in range(PASSES)
         ]
 
-        def project(gh):
-            for i in list(range(SRC_TILES, TOKEN_TILES)) + list(range(SRC_TILES)):
-                name = "s" if i < SRC_TILES else "t"
-                if i < SRC_TILES:
-                    key_bank = s_banks[gh]
-                else:
-                    key_bank = psum_turn.tile([P, PACK, P], F32, tag="turned")
-                for j in range(PACK):
-                    cols = slice(j * P, (j + 1) * P)
-                    for g in range(PASSES):
-                        nc.tensor.matmul_mx(
-                            out=key_bank[:, j, :],
-                            lhsT=w_codes[(name, gh)][:, g, cols].bitcast(FP8X4),
-                            lhsT_scale=w_scales[(name, gh)][:, g, cols],
-                            rhs=token_codes[:, i, g, :].bitcast(FP8X4),
-                            rhs_scale=token_scales[:, i, g, :],
-                            start=(g == 0),
-                            stop=(g == PASSES - 1),
-                        )
-                by_row = key_bank[:].rearrange("p j r -> p r j")
-                if i < SRC_TILES:
-                    nc.vector.tensor_copy(out=s_keys[:, gh, :, :], in_=by_row)
-                else:
-                    rows = slice((i - SRC_TILES) * P, (i - SRC_TILES + 1) * P)
-                    nc.vector.tensor_tensor(
-                        out=t_keys[:, gh, rows, :],
-                        in0=by_row,
-                        in1=bias_sum[:, gh, :].unsqueeze(1).to_broadcast([P, P, PACK]),
-                        op=ADD,
+        key_banks = {}
+
+        def project(i, gh):
+            name = "s" if i < SRC_TILES else "t"
+            if i < SRC_TILES:
+                key_bank = s_banks[gh]
+            else:
+                key_bank = psum_turn.tile([P, PACK, P], F32, tag="turned")
+            key_banks[(i, gh)] = key_bank
+            for j in range(PACK):
+                cols = slice(j * P, (j + 1) * P)
+                for g in range(PASSES):
+                    nc.tensor.matmul_mx(
+                        out=key_bank[:, j, :],
+                        lhsT=w_codes[(name, gh)][:, g, cols].bitcast(FP8X4),
+                        lhsT_scale=w_scales[(name, gh)][:, g, cols],
+                        rhs=token_codes[:, i, g, :].bitcast(FP8X4),
+                        rhs_scale=token_scales[:, i, g, :],
+                        start=(g == 0),
+                        stop=(g == PASSES - 1),
                     )
+
+        def keep_keys(i, gh):
+            by_row = key_banks[(i, gh)][:].rearrange("p j r -> p r j")
+            if i < SRC_TILES:
+                nc.vector.tensor_copy(out=s_keys[:, gh, :, :], in_=by_row)
+            else:
+                rows = slice((i - SRC_TILES) * P, (i - SRC_TILES + 1) * P)
+                nc.vector.tensor_tensor(
+                    out=t_keys[:, gh, rows, :],
+                    in0=by_row,
+                    in1=bias_sum[:, gh, :].unsqueeze(1).to_broadcast([P, P, PACK]),
+                    op=ADD,
+                )
 
         q_codes = keep.tile([P, B * L_TILES, PASSES, P], U32, align_bytes=64)
         q_scales = keep.tile([P, B * L_TILES, PASSES, P], U8, align_bytes=64)
-        q_grouped = keep.tile([P, B * L_TILES, PASSES, P, PACK], BF16, align_bytes=64)
+        q_grouped = {}
+
+        q_banks = {}
 
         def turn_q(b):
             for i in range(L_TILES):
                 bank = psum_acc.tile([P, PASSES * 2, P], F32, tag="acc%d" % i)
-                tile_index = b * L_TILES + i
-                turn_rows(nc, bank, ident[:], q_rows[b][:, i, :], q_grouped[:, tile_index])
+                turn_rows(nc, bank, ident[:], q_rows[b][:, i, :])
+                q_banks[(b, i)] = bank
+
+        def group_q(b):
+            q_grouped[b] = stage.tile(
+                [P, L_TILES, PASSES, P, PACK], BF16, align_bytes=64, tag="grouped", name="q_grouped"
+            )
+            for i in range(L_TILES):
+                group_rows(nc.scalar.copy, q_banks[(b, i)], q_grouped[b][:, i])
 
         def quantise_q(b):
             tiles = slice(b * L_TILES, (b + 1) * L_TILES)
             nc.vector.quantize_mx(
                 out=q_codes[:, tiles].rearrange("p i g r -> p (i g r)").bitcast(FP8X4),
                 scales=q_scales[:, tiles].rearrange("p i g r -> p (i g r)"),
-                in_=q_grouped[:, tiles].rearrange("p i g r j -> p (i g r j)"),
+                in_=q_grouped[b][:].rearrange("p i g r j -> p (i g r j)"),
             )
 
-        units = [(b, c, gh) for b in range(B) for c in range(T // T_CHUNK) for gh in range(PASSES)]
+        units = [
+            (b, c, gh) for b in range(B) for c in range(T // T_CHUNK) for gh in range(PASSES)
+        ]
         key_sums = {}
         rels = {}
         accs = {}
@@ -225,6 +245,8 @@ def tile_dynamicattention4_pa_kernel(tc, q, src, trg, Ws, b_s, Wt, b_t, out):
             b, c, gh = units[n]
             src_rows = slice(b * S, (b + 1) * S)
             first_t = b * T + c * T_CHUNK
+            sum_g = work.tile([P, T_GPSIMD, S, PACK], F32)
+            nc.vector.memset(sum_g[:, 0:1, 0:1, 0:1], 0.0)
             sum_v = work.tile([P, T_VECTOR, S, PACK], F32)
             nc.vector.tensor_tensor(
                 out=sum_v[:],
@@ -237,7 +259,6 @@ def tile_dynamicattention4_pa_kernel(tc, q, src, trg, Ws, b_s, Wt, b_t, out):
                 .to_broadcast([P, T_VECTOR, S, PACK]),
                 op=ADD,
             )
-            sum_g = work.tile([P, T_GPSIMD, S, PACK], F32)
             nc.gpsimd.tensor_tensor(
                 out=sum_g[:],
                 in0=s_keys[:, gh, src_rows, :].unsqueeze(1).to_broadcast([P, T_GPSIMD, S, PACK]),
@@ -258,72 +279,116 @@ def tile_dynamicattention4_pa_kernel(tc, q, src, trg, Ws, b_s, Wt, b_t, out):
             nc.scalar.activation(
                 out=rel[:, :split], in_=sum_v[:].rearrange("p t s j -> p (t s j)"), func=TANH
             )
-            rels[n] = rel
+            rels[units[n]] = rel
 
-        def multiply(n):
-            b, c, gh = units[n]
-            rel_codes = work.tile([P, N_COLS], U32, align_bytes=64)
-            rel_scales = work.tile([P, N_COLS], U8, align_bytes=64)
+        codes = {}
+        scores = {}
+
+        def quantise(unit):
+            rel_codes = work.tile([P, N_COLS], U32, align_bytes=64, bufs=4)
+            rel_scales = work.tile([P, N_COLS], U8, align_bytes=64, bufs=4)
             nc.vector.quantize_mx(
-                out=rel_codes[:].bitcast(FP8X4), scales=rel_scales[:], in_=rels[n][:]
+                out=rel_codes[:].bitcast(FP8X4), scales=rel_scales[:], in_=rels[unit][:]
             )
+            codes[unit] = (rel_codes, rel_scales)
+
+        def multiply(unit, i):
+            b, c, gh = unit
+            rel_codes, rel_scales = codes[unit]
             if gh == 0:
-                accs[(b, c)] = [
-                    psum_acc.tile([P, N_COLS], F32, name="acc%d" % i) for i in range(L_TILES)
-                ]
-            for i in range(L_TILES):
-                nc.tensor.matmul_mx(
-                    out=accs[(b, c)][i][:],
-                    lhsT=q_codes[:, b * L_TILES + i, gh, :].bitcast(FP8X4),
-                    lhsT_scale=q_scales[:, b * L_TILES + i, gh, :],
-                    rhs=rel_codes[:].bitcast(FP8X4),
-                    rhs_scale=rel_scales[:],
-                    start=(gh == 0),
-                    stop=(gh == PASSES - 1),
-                )
-
-        def store_scores(n):
-            b, c, gh = units[n]
-            acc = accs[(b, c)]
-            scores = work.tile([P, L_TILES, N_COLS], F32)
-            nc.scalar.mul(out=scores[:, 0, :], in_=acc[0][:], mul=H ** -0.5)
-            nc.vector.tensor_scalar_mul(out=scores[:, 1, :], in0=acc[1][:], scalar1=H ** -0.5)
-            nc.sync.dma_start(
-                out=out[b].rearrange("(i p) t s -> p i (t s)", p=P)[
-                    :, :, c * N_COLS : (c + 1) * N_COLS
-                ],
-                in_=scores[:],
+                accs[(b, c, i)] = psum_acc.tile([P, N_COLS], F32, name="acc%d" % i)
+            nc.tensor.matmul_mx(
+                out=accs[(b, c, i)][:],
+                lhsT=q_codes[:, b * L_TILES + i, gh, :].bitcast(FP8X4),
+                lhsT_scale=q_scales[:, b * L_TILES + i, gh, :],
+                rhs=rel_codes[:].bitcast(FP8X4),
+                rhs_scale=rel_scales[:],
+                start=(gh == 0),
+                stop=(gh == PASSES - 1),
             )
 
-        regroup_weight_columns("t", 0)
-        quantise_weight_columns("t", 0)
-        quantise_tokens()
-        regroup_weight_columns("s", 0)
-        quantise_weight_columns("s", 0)
+        def scale_scores(unit, i, engine_mul, cols):
+            key = unit + (i,)
+            if key not in scores:
+                scores[key] = work.tile([P, N_COLS], F32, bufs=4, name="scores")
+            b, c, gh = unit
+            engine_mul(scores[key][:, cols], accs[(b, c, i)][:, cols], H ** -0.5)
+
+        def store_scores(unit, i):
+            b, c, gh = unit
+            nc.sync.dma_start(
+                out=out[b, i * P : (i + 1) * P].rearrange("p t s -> p (t s)")[
+                    :, c * N_COLS : (c + 1) * N_COLS
+                ],
+                in_=scores[unit + (i,)][:],
+            )
+
+        for g in range(PASSES):
+            regroup_s("t", 0, g)
+            regroup_v("t", 0, g)
+        for g in range(PASSES):
+            quantise_weight("t", 0, g)
+        for i in range(TOKEN_TILES):
+            turn_token(i)
+        for i in range(TOKEN_TILES):
+            quantise_token(i)
+        for g in range(PASSES):
+            regroup_s("s", 0, g)
+            regroup_v("s", 0, g)
+        for g in range(PASSES):
+            quantise_weight("s", 0, g)
         turn_biases()
-        project(0)
+        for i in (1, 2, 0):
+            project(i, 0)
+        regroup_s("t", 1, 0)
+        regroup_v("t", 1, 0)
+        regroup_s("t", 1, 1)
+        for i in (1, 2, 0):
+            keep_keys(i, 0)
         add_keys(0)
-        regroup_weight_columns("t", 1)
-        regroup_weight_columns("s", 1)
-        take_tanh(0)
+        regroup_v("t", 1, 1)
         turn_q(0)
         turn_q(1)
-        quantise_weight_columns("t", 1)
-        quantise_weight_columns("s", 1)
-        project(1)
+        regroup_s("s", 1, 0)
+        regroup_s("s", 1, 1)
+        for g in range(PASSES):
+            quantise_weight("t", 1, g)
+        for g in range(PASSES):
+            regroup_v("s", 1, g)
+        take_tanh(0)
+        for g in range(PASSES):
+            quantise_weight("s", 1, g)
+        for i in (1, 2, 0):
+            project(i, 1)
+        group_q(0)
+        group_q(1)
         turn_q(2)
         turn_q(3)
+        for i in (1, 2, 0):
+            keep_keys(i, 1)
         quantise_q(0)
+        group_q(2)
+        group_q(3)
 
-        units_per_batch = len(units) // B
-        for n in range(1, len(units) + 3):
+        last = PASSES - 1
+        mul_s = nc.scalar.mul
+        mul_v = nc.vector.tensor_scalar_mul
+        low, high = slice(0, N_COLS // 2), slice(N_COLS // 2, N_COLS)
+        for n in range(1, len(units) + 5):
             if n < len(units):
                 add_keys(n)
+            if 0 <= n - 3 < len(units) and units[n - 3][2] == last:
+                scale_scores(units[n - 3], 0, mul_s, slice(0, N_COLS))
+                store_scores(units[n - 3], 0)
+                scale_scores(units[n - 3], 1, mul_v, low)
+            if 0 <= n - 4 < len(units) and units[n - 4][2] == last:
+                scale_scores(units[n - 4], 1, mul_v, high)
+                store_scores(units[n - 4], 1)
             if 0 <= n - 2 < len(units):
-                multiply(n - 2)
-            if 0 <= n - 3 and units[n - 3][2] == PASSES - 1:
-                store_scores(n - 3)
+                quantise(units[n - 2])
+                for i in range(L_TILES):
+                    multiply(units[n - 2], i)
             if n < len(units):
                 take_tanh(n)
-                if n % units_per_batch == 1 and n // units_per_batch + 1 < B:
-                    quantise_q(n // units_per_batch + 1)
+                if n % 8 == 1 and n // 8 + 1 < B:
+                    quantise_q(n // 8 + 1)

@@ -20,6 +20,7 @@ T_CHUNK = 16
 N_COLS = T_CHUNK * S
 T_GPSIMD = 5
 T_VECTOR = T_CHUNK - T_GPSIMD
+RING = 5
 L_TILES = L // P
 SRC_TILES = B * S // P
 TOKEN_TILES = SRC_TILES + B * T // P
@@ -43,6 +44,7 @@ def tile_dynamicattention4_pa_kernel(tc, q, src, trg, Ws, b_s, Wt, b_t, out):
         keep = ctx.enter_context(tc.tile_pool(name="keep", bufs=1))
         stage = ctx.enter_context(tc.tile_pool(name="stage", bufs=6))
         work = ctx.enter_context(tc.tile_pool(name="work", bufs=3))
+        ring = ctx.enter_context(tc.tile_pool(name="ring", bufs=1))
         psum_turn = ctx.enter_context(tc.psum_pool(name="psum_turn", bufs=2))
         psum_src = ctx.enter_context(tc.psum_pool(name="psum_src", bufs=1))
         psum_acc = ctx.enter_context(tc.psum_pool(name="psum_acc", bufs=2))
@@ -120,11 +122,11 @@ def tile_dynamicattention4_pa_kernel(tc, q, src, trg, Ws, b_s, Wt, b_t, out):
                 in_=w_rows[key][:, :, half].rearrange("p j (c e) -> p e c j", e=2),
             )
 
-        def regroup_v(name, gh, g):
-            regroup(nc.vector.tensor_copy, 0, name, gh, g)
+        def regroup_v(name, gh, g, u=0):
+            regroup(nc.vector.tensor_copy, u, name, gh, g)
 
-        def regroup_s(name, gh, g):
-            regroup(nc.scalar.copy, 1, name, gh, g)
+        def regroup_d(name, gh, g, u=1):
+            regroup(nc.scalar.copy, u, name, gh, g)
 
         def quantise_weight(name, gh, g):
             nc.vector.quantize_mx(
@@ -213,18 +215,21 @@ def tile_dynamicattention4_pa_kernel(tc, q, src, trg, Ws, b_s, Wt, b_t, out):
 
         q_banks = {}
 
-        def turn_q(b):
-            for i in range(L_TILES):
-                bank = psum_acc.tile([P, PASSES * 2, P], F32, tag="acc%d" % i)
-                turn_rows(nc, bank, ident[:], q_rows[b][:, i, :])
-                q_banks[(b, i)] = bank
+        def turn_q(b, i):
+            bank = psum_turn.tile([P, PASSES * 2, P], F32, tag="turned")
+            turn_rows(nc, bank, ident[:], q_rows[b][:, i, :])
+            q_banks[(b, i)] = bank
 
-        def group_q(b):
-            q_grouped[b] = stage.tile(
-                [P, L_TILES, PASSES, P, PACK], BF16, align_bytes=64, tag="grouped", name="q_grouped"
-            )
-            for i in range(L_TILES):
-                group_rows(nc.scalar.copy, q_banks[(b, i)], q_grouped[b][:, i])
+        def group_q(copy, b, i):
+            if i == 0:
+                q_grouped[b] = stage.tile(
+                    [P, L_TILES, PASSES, P, PACK],
+                    BF16,
+                    align_bytes=64,
+                    tag="grouped",
+                    name="q_grouped",
+                )
+            group_rows(copy, q_banks[(b, i)], q_grouped[b][:, i])
 
         def quantise_q(b):
             tiles = slice(b * L_TILES, (b + 1) * L_TILES)
@@ -237,6 +242,7 @@ def tile_dynamicattention4_pa_kernel(tc, q, src, trg, Ws, b_s, Wt, b_t, out):
         units = [
             (b, c, gh) for b in range(B) for c in range(T // T_CHUNK) for gh in range(PASSES)
         ]
+        units[1], units[2] = units[2], units[1]
         key_sums = {}
         rels = {}
         accs = {}
@@ -245,8 +251,7 @@ def tile_dynamicattention4_pa_kernel(tc, q, src, trg, Ws, b_s, Wt, b_t, out):
             b, c, gh = units[n]
             src_rows = slice(b * S, (b + 1) * S)
             first_t = b * T + c * T_CHUNK
-            sum_g = work.tile([P, T_GPSIMD, S, PACK], F32)
-            nc.vector.memset(sum_g[:, 0:1, 0:1, 0:1], 0.0)
+            sum_g = ring.tile([P, T_GPSIMD, S, PACK], F32, name="ring%d" % (2 * n % RING), align_bytes=64)
             sum_v = work.tile([P, T_VECTOR, S, PACK], F32)
             nc.vector.tensor_tensor(
                 out=sum_v[:],
@@ -271,7 +276,9 @@ def tile_dynamicattention4_pa_kernel(tc, q, src, trg, Ws, b_s, Wt, b_t, out):
 
         def take_tanh(n):
             sum_v, sum_g = key_sums[n]
-            rel = work.tile([P, N_COLS * PACK], BF16, align_bytes=64)
+            rel = ring.tile(
+                [P, N_COLS * PACK], BF16, name="ring%d" % ((2 * n + 1) % RING), align_bytes=64
+            )
             split = T_VECTOR * S * PACK
             nc.scalar.activation(
                 out=rel[:, split:], in_=sum_g[:].rearrange("p t s j -> p (t s j)"), func=TANH
@@ -324,7 +331,7 @@ def tile_dynamicattention4_pa_kernel(tc, q, src, trg, Ws, b_s, Wt, b_t, out):
             )
 
         for g in range(PASSES):
-            regroup_s("t", 0, g)
+            regroup_d("t", 0, g)
             regroup_v("t", 0, g)
         for g in range(PASSES):
             quantise_weight("t", 0, g)
@@ -332,63 +339,75 @@ def tile_dynamicattention4_pa_kernel(tc, q, src, trg, Ws, b_s, Wt, b_t, out):
             turn_token(i)
         for i in range(TOKEN_TILES):
             quantise_token(i)
+        turn_biases()
         for g in range(PASSES):
-            regroup_s("s", 0, g)
+            regroup_d("s", 0, g)
             regroup_v("s", 0, g)
+        for i in (1, 2):
+            project(i, 0)
         for g in range(PASSES):
             quantise_weight("s", 0, g)
-        turn_biases()
-        for i in (1, 2, 0):
-            project(i, 0)
-        regroup_s("t", 1, 0)
-        regroup_v("t", 1, 0)
-        regroup_s("t", 1, 1)
+        project(0, 0)
+        for g in range(PASSES):
+            regroup_d("t", 1, g)
         for i in (1, 2, 0):
             keep_keys(i, 0)
         add_keys(0)
-        regroup_v("t", 1, 1)
-        turn_q(0)
-        turn_q(1)
-        regroup_s("s", 1, 0)
-        regroup_s("s", 1, 1)
+        for g in range(PASSES):
+            regroup_v("t", 1, g)
         for g in range(PASSES):
             quantise_weight("t", 1, g)
-        for g in range(PASSES):
-            regroup_v("s", 1, g)
+        add_keys(1)
         take_tanh(0)
         for g in range(PASSES):
-            quantise_weight("s", 1, g)
-        for i in (1, 2, 0):
+            regroup_d("s", 1, g)
+            regroup_v("s", 1, g)
+        for i in (1, 2):
             project(i, 1)
-        group_q(0)
-        group_q(1)
-        turn_q(2)
-        turn_q(3)
+        for g in range(PASSES):
+            quantise_weight("s", 1, g)
+        project(0, 1)
+        take_tanh(1)
+        for i in range(L_TILES):
+            turn_q(0, i)
         for i in (1, 2, 0):
             keep_keys(i, 1)
-        quantise_q(0)
-        group_q(2)
-        group_q(3)
+        for i in range(L_TILES):
+            group_q(nc.scalar.copy, 0, i)
 
         last = PASSES - 1
         mul_s = nc.scalar.mul
         mul_v = nc.vector.tensor_scalar_mul
-        low, high = slice(0, N_COLS // 2), slice(N_COLS // 2, N_COLS)
-        for n in range(1, len(units) + 5):
+        late_q = {4: (1, 0), 5: (1, 1), 11: (2, 0), 13: (2, 1), 19: (3, 0), 21: (3, 1)}
+        final = len(units) - 1
+        for n in range(2, len(units) + 4):
             if n < len(units):
                 add_keys(n)
-            if 0 <= n - 3 < len(units) and units[n - 3][2] == last:
-                scale_scores(units[n - 3], 0, mul_s, slice(0, N_COLS))
-                store_scores(units[n - 3], 0)
-                scale_scores(units[n - 3], 1, mul_v, low)
-            if 0 <= n - 4 < len(units) and units[n - 4][2] == last:
-                scale_scores(units[n - 4], 1, mul_v, high)
+            if n in late_q:
+                turn_q(*late_q[n])
+            if 0 <= n - 3 < final and units[n - 3][2] == last:
+                scale_scores(units[n - 3], 0, mul_s, slice(0, 384))
+                scale_scores(units[n - 3], 1, mul_v, slice(0, 320))
+            if 0 <= n - 4 < final and units[n - 4][2] == last:
+                scale_scores(units[n - 4], 1, mul_v, slice(320, N_COLS))
                 store_scores(units[n - 4], 1)
-            if 0 <= n - 2 < len(units):
+                scale_scores(units[n - 4], 0, mul_v, slice(384, N_COLS))
+                store_scores(units[n - 4], 0)
+            if n - 3 == final:
+                scale_scores(units[final], 0, mul_s, slice(0, N_COLS))
+                scale_scores(units[final], 1, mul_v, slice(0, N_COLS))
+                store_scores(units[final], 0)
+                store_scores(units[final], 1)
+            if n == 2:
+                quantise_q(0)
+            if n - 2 < len(units):
                 quantise(units[n - 2])
                 for i in range(L_TILES):
                     multiply(units[n - 2], i)
             if n < len(units):
                 take_tanh(n)
-                if n % 8 == 1 and n // 8 + 1 < B:
-                    quantise_q(n // 8 + 1)
+            if n in late_q:
+                b, i = late_q[n]
+                group_q(nc.scalar.copy, b, i)
+            if n - 3 in late_q and late_q[n - 3][1] == 1:
+                quantise_q(late_q[n - 3][0])

@@ -7,6 +7,7 @@ F32 = mybir.dt.float32
 BF16 = mybir.dt.bfloat16
 U32 = mybir.dt.uint32
 U8 = mybir.dt.uint8
+I32 = mybir.dt.int32
 FP8X4 = mybir.dt.float8_e4m3fn_x4
 ADD = mybir.AluOpType.add
 TANH = mybir.ActivationFunctionType.Tanh
@@ -18,8 +19,12 @@ K_PASS = P * PACK
 PASSES = F // K_PASS
 T_CHUNK = 16
 N_COLS = T_CHUNK * S
-T_GPSIMD = 5
+T_GPSIMD = 6
 T_VECTOR = T_CHUNK - T_GPSIMD
+B_PE = 1
+BLOCK_T = 4
+BLOCK_COLS = BLOCK_T * S
+BLOCKS = T_CHUNK // BLOCK_T
 RING = 5
 L_TILES = L // P
 SRC_TILES = B * S // P
@@ -47,7 +52,7 @@ def tile_dynamicattention4_pa_kernel(tc, q, src, trg, Ws, b_s, Wt, b_t, out):
         ring = ctx.enter_context(tc.tile_pool(name="ring", bufs=1))
         psum_turn = ctx.enter_context(tc.psum_pool(name="psum_turn", bufs=2))
         psum_src = ctx.enter_context(tc.psum_pool(name="psum_src", bufs=1))
-        psum_acc = ctx.enter_context(tc.psum_pool(name="psum_acc", bufs=2))
+        psum_acc = ctx.enter_context(tc.psum_pool(name="psum_acc", bufs=1))
         ctx.enter_context(tc.manual_schedule())
 
         ident = keep.tile([P, P], F32)
@@ -64,6 +69,30 @@ def tile_dynamicattention4_pa_kernel(tc, q, src, trg, Ws, b_s, Wt, b_t, out):
             out=bias_rows[bias_row_count : 2 * bias_row_count, :],
             in_=b_t.rearrange("(r c) -> r c", c=2 * P),
         )
+
+        bias_flat = keep.tile([P, H], BF16)
+        nc.gpsimd.memset(bias_flat[:], 0.0)
+        nc.gpsimd.dma_start(out=bias_flat[0:1, :], in_=b_s.rearrange("(r c) -> r c", r=1))
+        nc.gpsimd.dma_start(out=bias_flat[1:2, :], in_=b_t.rearrange("(r c) -> r c", r=1))
+
+        pick = keep.tile([P, T, S], F32)
+        pick_s = keep.tile([P, S], F32)
+        nc.vector.tensor_copy(out=pick_s[:], in_=ident[:, S : 2 * S])
+        nc.vector.memset(pick_s[0:S, :], 1.0)
+        nc.vector.tensor_tensor(
+            out=pick[:],
+            in0=pick_s[:].unsqueeze(1).to_broadcast([P, T, S]),
+            in1=ident[:, 2 * S :].unsqueeze(2).to_broadcast([P, T, S]),
+            op=ADD,
+        )
+
+        pe_codes = {}
+        pe_scales = {}
+        for name in ("s", "t"):
+            pe_codes[name] = keep.tile([P, PASSES, P], U32, name="pe_codes_%s" % name, align_bytes=64)
+            pe_scales[name] = keep.tile([P, PASSES, P], U8, name="pe_scales_%s" % name, align_bytes=64)
+            nc.gpsimd.memset(pe_codes[name][:], 0)
+            nc.gpsimd.memset(pe_scales[name][:].bitcast(U32), 0)
 
         weights = {"s": Ws, "t": Wt}
         w_rows = {}
@@ -95,7 +124,7 @@ def tile_dynamicattention4_pa_kernel(tc, q, src, trg, Ws, b_s, Wt, b_t, out):
         load_weight_columns("t", 1)
         load_weight_columns("s", 1)
         q_rows = [keep.tile([P, L_TILES, H], BF16, name="q_rows%d" % b) for b in range(B)]
-        for b in range(B):
+        for b in (0, B_PE, 2, 3):
             nc.sync.dma_start(out=q_rows[b][:], in_=q[b].rearrange("(i p) h -> p i h", p=P))
 
         w_codes = {}
@@ -151,6 +180,19 @@ def tile_dynamicattention4_pa_kernel(tc, q, src, trg, Ws, b_s, Wt, b_t, out):
                 in_=token_grouped[:, i].rearrange("p g r j -> p (g r j)"),
             )
 
+        def pick_pe_codes():
+            for name, tile_index, cols in (
+                ("s", 0, slice(S, 2 * S)),
+                ("t", SRC_TILES, slice(2 * S, 2 * S + T)),
+            ):
+                nc.vector.tensor_copy(
+                    out=pe_codes[name][:, :, cols].bitcast(I32),
+                    in_=token_codes[:, tile_index, :, cols].bitcast(I32),
+                )
+                nc.vector.tensor_copy(
+                    out=pe_scales[name][:, :, cols], in_=token_scales[:, tile_index, :, cols]
+                )
+
         bias_sum = keep.tile([P, PASSES, PACK], F32)
 
         def turn_biases():
@@ -176,12 +218,15 @@ def tile_dynamicattention4_pa_kernel(tc, q, src, trg, Ws, b_s, Wt, b_t, out):
 
         key_banks = {}
 
-        def project(i, gh):
+        def project(i, gh, tag=None):
             name = "s" if i < SRC_TILES else "t"
             if i < SRC_TILES:
                 key_bank = s_banks[gh]
             else:
-                key_bank = psum_turn.tile([P, PACK, P], F32, tag="turned")
+                if tag is None:
+                    key_bank = psum_turn.tile([P, PACK, P], F32, tag="turned")
+                else:
+                    key_bank = psum_acc.tile([P, PACK, P], F32, tag=tag)
             key_banks[(i, gh)] = key_bank
             for j in range(PACK):
                 cols = slice(j * P, (j + 1) * P)
@@ -199,7 +244,7 @@ def tile_dynamicattention4_pa_kernel(tc, q, src, trg, Ws, b_s, Wt, b_t, out):
         def keep_keys(i, gh):
             by_row = key_banks[(i, gh)][:].rearrange("p j r -> p r j")
             if i < SRC_TILES:
-                nc.vector.tensor_copy(out=s_keys[:, gh, :, :], in_=by_row)
+                nc.scalar.copy(out=s_keys[:, gh, :, :], in_=by_row)
             else:
                 rows = slice((i - SRC_TILES) * P, (i - SRC_TILES + 1) * P)
                 nc.vector.tensor_tensor(
@@ -209,14 +254,46 @@ def tile_dynamicattention4_pa_kernel(tc, q, src, trg, Ws, b_s, Wt, b_t, out):
                     op=ADD,
                 )
 
+        pe_keys = keep.tile([P, PASSES, K_PASS], F32)
+        row_banks = {}
+
+        def project_rows(gh, tag=None):
+            if tag is None:
+                bank = psum_turn.tile([P, K_PASS], F32, tag="turned")
+            else:
+                bank = psum_acc.tile([P, K_PASS], F32, tag=tag)
+            steps = [(name, g) for name in ("t", "s") for g in range(PASSES)]
+            for name, g in steps:
+                nc.tensor.matmul_mx(
+                    out=bank[:],
+                    lhsT=pe_codes[name][:, g, :].bitcast(FP8X4),
+                    lhsT_scale=pe_scales[name][:, g, :],
+                    rhs=w_codes[(name, gh)][:, g, :].bitcast(FP8X4),
+                    rhs_scale=w_scales[(name, gh)][:, g, :],
+                    start=((name, g) == steps[0]),
+                    stop=((name, g) == steps[-1]),
+                )
+            row_banks[gh] = bank
+
+        def keep_rows(gh):
+            nc.vector.tensor_tensor(
+                out=pe_keys[:, gh, :].rearrange("p (u e c) -> p u e c", u=2, e=2),
+                in0=row_banks[gh][:].rearrange("p (u e c) -> p u e c", u=2, e=2),
+                in1=bias_flat[:, gh * K_PASS : (gh + 1) * K_PASS].rearrange(
+                    "p (u c e) -> p u e c", u=2, e=2
+                ),
+                op=ADD,
+            )
+
         q_codes = keep.tile([P, B * L_TILES, PASSES, P], U32, align_bytes=64)
         q_scales = keep.tile([P, B * L_TILES, PASSES, P], U8, align_bytes=64)
         q_grouped = {}
 
         q_banks = {}
 
-        def turn_q(b, i):
-            bank = psum_turn.tile([P, PASSES * 2, P], F32, tag="turned")
+        def turn_q(b, i, bank=None):
+            if bank is None:
+                bank = psum_acc.tile([P, PASSES * 2, P], F32, tag="acc%d%d" % (b == B_PE, i))
             turn_rows(nc, bank, ident[:], q_rows[b][:, i, :])
             q_banks[(b, i)] = bank
 
@@ -239,15 +316,16 @@ def tile_dynamicattention4_pa_kernel(tc, q, src, trg, Ws, b_s, Wt, b_t, out):
                 in_=q_grouped[b][:].rearrange("p i g r j -> p (i g r j)"),
             )
 
-        units = [
-            (b, c, gh) for b in range(B) for c in range(T // T_CHUNK) for gh in range(PASSES)
-        ]
+        pairs = [(c, gh) for c in range(T // T_CHUNK) for gh in range(PASSES)]
+        units = [(b, c, gh) for b in range(B) if b != B_PE for c, gh in pairs]
+        units.append((B_PE,) + pairs[-1])
         units[1], units[2] = units[2], units[1]
+        pe_units = [(B_PE, c, gh) for c, gh in pairs[:-1]]
         key_sums = {}
         rels = {}
         accs = {}
 
-        def add_keys(n):
+        def add_keys(n, vector_alone=False):
             b, c, gh = units[n]
             src_rows = slice(b * S, (b + 1) * S)
             first_t = b * T + c * T_CHUNK
@@ -264,9 +342,15 @@ def tile_dynamicattention4_pa_kernel(tc, q, src, trg, Ws, b_s, Wt, b_t, out):
                 .to_broadcast([P, T_VECTOR, S, PACK]),
                 op=ADD,
             )
-            nc.gpsimd.tensor_tensor(
+            if vector_alone:
+                other = nc.vector
+                src_keys = s_banks[gh][:, :, src_rows].rearrange("p j s -> p s j")
+            else:
+                other = nc.gpsimd
+                src_keys = s_keys[:, gh, src_rows, :]
+            other.tensor_tensor(
                 out=sum_g[:],
-                in0=s_keys[:, gh, src_rows, :].unsqueeze(1).to_broadcast([P, T_GPSIMD, S, PACK]),
+                in0=src_keys.unsqueeze(1).to_broadcast([P, T_GPSIMD, S, PACK]),
                 in1=t_keys[:, gh, first_t + T_VECTOR : first_t + T_CHUNK, :]
                 .unsqueeze(2)
                 .to_broadcast([P, T_GPSIMD, S, PACK]),
@@ -274,60 +358,99 @@ def tile_dynamicattention4_pa_kernel(tc, q, src, trg, Ws, b_s, Wt, b_t, out):
             )
             key_sums[n] = (sum_v, sum_g)
 
-        def take_tanh(n):
+        split = T_VECTOR * S
+
+        def take_tanh(n, first, stop):
             sum_v, sum_g = key_sums[n]
-            rel = ring.tile(
-                [P, N_COLS * PACK], BF16, name="ring%d" % ((2 * n + 1) % RING), align_bytes=64
-            )
-            split = T_VECTOR * S * PACK
+            if units[n] not in rels:
+                rels[units[n]] = ring.tile(
+                    [P, N_COLS * PACK],
+                    BF16,
+                    name="ring%d" % ((2 * n + 1) % RING),
+                    align_bytes=64,
+                )
+            sums, start = (sum_v, 0) if stop <= split else (sum_g, split)
             nc.scalar.activation(
-                out=rel[:, split:], in_=sum_g[:].rearrange("p t s j -> p (t s j)"), func=TANH
+                out=rels[units[n]][:, first * PACK : stop * PACK],
+                in_=sums[:].rearrange("p t s j -> p (t s j)")[
+                    :, (first - start) * PACK : (stop - start) * PACK
+                ],
+                func=TANH,
             )
+
+        blocks = [(unit, k) for unit in pe_units for k in range(BLOCKS)]
+        block_banks = {}
+
+        def add_block(m):
+            (b, c, gh), k = blocks[m]
+            bank = psum_turn.tile([P, PACK, BLOCK_COLS], F32, tag="turned")
+            first_t = c * T_CHUNK + k * BLOCK_T
+            for j in range(PACK):
+                nc.tensor.matmul(
+                    out=bank[:, j, :],
+                    lhsT=pe_keys[:, gh, j * P : (j + 1) * P],
+                    rhs=pick[:, first_t : first_t + BLOCK_T, :].rearrange("p t s -> p (t s)"),
+                    start=True,
+                    stop=True,
+                )
+            block_banks[m] = bank
+
+        def take_block_tanh(m):
+            unit, k = blocks[m]
+            if k == 0:
+                rels[unit] = work.tile([P, N_COLS * PACK], BF16, align_bytes=64, name="rel_pe")
+            cols = slice(k * BLOCK_COLS * PACK, (k + 1) * BLOCK_COLS * PACK)
             nc.scalar.activation(
-                out=rel[:, :split], in_=sum_v[:].rearrange("p t s j -> p (t s j)"), func=TANH
+                out=rels[unit][:, cols].rearrange("p (c j) -> p c j", j=PACK),
+                in_=block_banks[m][:].rearrange("p j c -> p c j"),
+                func=TANH,
             )
-            rels[units[n]] = rel
 
         codes = {}
-        scores = {}
 
-        def quantise(unit):
-            rel_codes = work.tile([P, N_COLS], U32, align_bytes=64, bufs=4)
-            rel_scales = work.tile([P, N_COLS], U8, align_bytes=64, bufs=4)
+        whole = slice(0, N_COLS)
+
+        def quantise(unit, cols=whole):
+            if unit not in codes:
+                rel_codes = work.tile([P, N_COLS], U32, align_bytes=64, bufs=6)
+                rel_scales = work.tile([P, N_COLS], U8, align_bytes=64, bufs=6)
+                codes[unit] = (rel_codes, rel_scales)
             nc.vector.quantize_mx(
-                out=rel_codes[:].bitcast(FP8X4), scales=rel_scales[:], in_=rels[unit][:]
+                out=codes[unit][0][:, cols].bitcast(FP8X4),
+                scales=codes[unit][1][:, cols],
+                in_=rels[unit][:, cols.start * PACK : cols.stop * PACK],
             )
-            codes[unit] = (rel_codes, rel_scales)
 
-        def multiply(unit, i):
+        def multiply(unit, i, cols=whole):
             b, c, gh = unit
             rel_codes, rel_scales = codes[unit]
-            if gh == 0:
-                accs[(b, c, i)] = psum_acc.tile([P, N_COLS], F32, name="acc%d" % i)
+            if (b, c, i) not in accs:
+                accs[(b, c, i)] = psum_acc.tile([P, N_COLS], F32, name="acc%d%d" % (b == B_PE, i))
             nc.tensor.matmul_mx(
-                out=accs[(b, c, i)][:],
+                out=accs[(b, c, i)][:, cols],
                 lhsT=q_codes[:, b * L_TILES + i, gh, :].bitcast(FP8X4),
                 lhsT_scale=q_scales[:, b * L_TILES + i, gh, :],
-                rhs=rel_codes[:].bitcast(FP8X4),
-                rhs_scale=rel_scales[:],
+                rhs=rel_codes[:, cols].bitcast(FP8X4),
+                rhs_scale=rel_scales[:, cols],
                 start=(gh == 0),
                 stop=(gh == PASSES - 1),
             )
 
-        def scale_scores(unit, i, engine_mul, cols):
-            key = unit + (i,)
-            if key not in scores:
-                scores[key] = work.tile([P, N_COLS], F32, bufs=4, name="scores")
-            b, c, gh = unit
-            engine_mul(scores[key][:, cols], accs[(b, c, i)][:, cols], H ** -0.5)
+        scores = {}
 
-        def store_scores(unit, i):
+        def scale_scores(mul, unit, i, cols=whole):
+            b, c, gh = unit
+            if (unit, i) not in scores:
+                scores[(unit, i)] = work.tile([P, N_COLS], F32, bufs=6, name="scores")
+            mul(scores[(unit, i)][:, cols], accs[(b, c, i)][:, cols], H ** -0.5)
+
+        def store_scores(unit, i, cols=whole):
             b, c, gh = unit
             nc.sync.dma_start(
                 out=out[b, i * P : (i + 1) * P].rearrange("p t s -> p (t s)")[
-                    :, c * N_COLS : (c + 1) * N_COLS
+                    :, c * N_COLS + cols.start : c * N_COLS + cols.stop
                 ],
-                in_=scores[unit + (i,)][:],
+                in_=scores[(unit, i)][:, cols],
             )
 
         for g in range(PASSES):
@@ -343,71 +466,135 @@ def tile_dynamicattention4_pa_kernel(tc, q, src, trg, Ws, b_s, Wt, b_t, out):
         for g in range(PASSES):
             regroup_d("s", 0, g)
             regroup_v("s", 0, g)
-        for i in (1, 2):
-            project(i, 0)
+        project(1, 0)
         for g in range(PASSES):
             quantise_weight("s", 0, g)
         project(0, 0)
         for g in range(PASSES):
             regroup_d("t", 1, g)
-        for i in (1, 2, 0):
-            keep_keys(i, 0)
-        add_keys(0)
-        for g in range(PASSES):
-            regroup_v("t", 1, g)
+        regroup_d("t", 1, 0, 0)
+        keep_keys(1, 0)
+        add_keys(0, True)
+        keep_keys(0, 0)
+        regroup_v("t", 1, 1)
+        pick_pe_codes()
         for g in range(PASSES):
             quantise_weight("t", 1, g)
+        project(1, 1)
+        project_rows(0, "acc10")
+        for i in range(L_TILES):
+            turn_q(0, i)
         add_keys(1)
-        take_tanh(0)
+        take_tanh(0, split, N_COLS)
+        take_tanh(0, 0, split)
         for g in range(PASSES):
             regroup_d("s", 1, g)
             regroup_v("s", 1, g)
-        for i in (1, 2):
-            project(i, 1)
         for g in range(PASSES):
             quantise_weight("s", 1, g)
         project(0, 1)
-        take_tanh(1)
-        for i in range(L_TILES):
-            turn_q(0, i)
-        for i in (1, 2, 0):
-            keep_keys(i, 1)
+        take_tanh(1, split, N_COLS)
+        take_tanh(1, 0, split)
+        keep_keys(1, 1)
+        keep_rows(0)
+        keep_keys(0, 1)
+        for m in (0, 1):
+            add_block(m)
+        project_rows(1, "acc11")
+        project(2, 0, "acc10")
         for i in range(L_TILES):
             group_q(nc.scalar.copy, 0, i)
 
         last = PASSES - 1
         mul_s = nc.scalar.mul
         mul_v = nc.vector.tensor_scalar_mul
-        late_q = {4: (1, 0), 5: (1, 1), 11: (2, 0), 13: (2, 1), 19: (3, 0), 21: (3, 1)}
+        quantise_at = {}
+        multiply_at = {}
+        scale_at = {}
         final = len(units) - 1
-        for n in range(2, len(units) + 4):
+
+        def plan(unit, ready, start):
+            quantise_at.setdefault(ready, []).append(unit)
+            for i in range(L_TILES):
+                at = start + i
+                multiply_at.setdefault(at, []).append((unit, i))
+                if unit[2] == last:
+                    scale_at.setdefault(at + 1, []).append((unit, i))
+
+        steps = range(2, len(units))
+        due = {n: range((n - 2) * len(blocks) // len(steps), (n - 1) * len(blocks) // len(steps)) for n in steps}
+        for n in steps:
+            for m in due[n]:
+                if m % BLOCKS == BLOCKS - 1:
+                    plan(pe_units[m // BLOCKS], n + 1, n + 1)
+        for n in range(final):
+            plan(units[n], n + 2, 5 if n == 1 else n + 2)
+
+        late_q = {
+            4: [(B_PE, 0, "acc11")],
+            5: [(B_PE, 1, "acc10"), (2, 0, "acc11")],
+            6: [(2, 1, "acc11")],
+            11: [(3, 0, "acc10")],
+            12: [(3, 1, "acc11")],
+        }
+        for n in range(2, final + 1):
+            if n == 4:
+                project(2, 1, "acc10")
+            for m in due.get(n, []):
+                take_block_tanh(m)
             if n < len(units):
                 add_keys(n)
-            if n in late_q:
-                turn_q(*late_q[n])
-            if 0 <= n - 3 < final and units[n - 3][2] == last:
-                scale_scores(units[n - 3], 0, mul_s, slice(0, 384))
-                scale_scores(units[n - 3], 1, mul_v, slice(0, 320))
-            if 0 <= n - 4 < final and units[n - 4][2] == last:
-                scale_scores(units[n - 4], 1, mul_v, slice(320, N_COLS))
-                store_scores(units[n - 4], 1)
-                scale_scores(units[n - 4], 0, mul_v, slice(384, N_COLS))
-                store_scores(units[n - 4], 0)
-            if n - 3 == final:
-                scale_scores(units[final], 0, mul_s, slice(0, N_COLS))
-                scale_scores(units[final], 1, mul_v, slice(0, N_COLS))
-                store_scores(units[final], 0)
-                store_scores(units[final], 1)
+            if n == 3:
+                keep_keys(2, 0)
+                keep_rows(1)
+            if n == 4:
+                keep_keys(2, 1)
+            for unit, i in scale_at.get(n, []):
+                scale_scores(mul_v, unit, i)
+                store_scores(unit, i)
+            for unit in quantise_at.get(n, []):
+                quantise(unit)
             if n == 2:
                 quantise_q(0)
-            if n - 2 < len(units):
-                quantise(units[n - 2])
-                for i in range(L_TILES):
-                    multiply(units[n - 2], i)
-            if n < len(units):
-                take_tanh(n)
-            if n in late_q:
-                b, i = late_q[n]
+            if n in (6, 8, 14):
+                quantise_q({6: B_PE, 8: 2, 14: 3}[n])
+            for b, i, tag in late_q.get(n, []):
+                turn_q(b, i, psum_acc.tile([P, PASSES * 2, P], F32, name=tag))
+            if n < final:
+                take_tanh(n, split, N_COLS)
+                take_tanh(n, 0, split)
+            for b, i, tag in late_q.get(n, []):
                 group_q(nc.scalar.copy, b, i)
-            if n - 3 in late_q and late_q[n - 3][1] == 1:
-                quantise_q(late_q[n - 3][0])
+            for unit, i in multiply_at.get(n, []):
+                multiply(unit, i)
+            for m in due.get(n, []):
+                if m + 2 < len(blocks):
+                    add_block(m + 2)
+
+        half, quarter = N_COLS // 2, N_COLS // 4
+        take_tanh(final, split, N_COLS)
+        take_tanh(final, half, split)
+        take_tanh(final, 0, quarter)
+        take_tanh(final, quarter, half)
+        before, opener = units[final - 1], pe_units[-1]
+        for unit, i in scale_at[final + 1]:
+            scale_scores(mul_v, unit, i)
+            store_scores(unit, i)
+        quantise(opener)
+        quantise(before)
+        for unit, i in multiply_at[final + 1]:
+            if unit != opener:
+                multiply(unit, i)
+        multiply(before, 1)
+        for cols in (slice(half, N_COLS), slice(0, quarter), slice(quarter, half)):
+            quantise(units[final], cols)
+            for i in range(L_TILES):
+                multiply(opener, i, cols)
+                multiply(units[final], i, cols)
+        for i, mul in enumerate((mul_s, mul_v)):
+            scale_scores(mul, before, i)
+            store_scores(before, i)
+        for cols in (slice(half, N_COLS), slice(0, half)):
+            for i, mul in enumerate((mul_s, mul_v)):
+                scale_scores(mul, units[final], i, cols)
+                store_scores(units[final], i, cols)

@@ -147,8 +147,8 @@ def tile_dynamicattention4_pa_kernel(tc, q, src, trg, Ws, b_s, Wt, b_t, out):
                 )
             half = slice(u * 2 * P, (u + 1) * 2 * P)
             copy(
-                out=w_grouped[key][:, half, :].rearrange("p (e c) j -> p e c j", e=2),
-                in_=w_rows[key][:, :, half].rearrange("p j (c e) -> p e c j", e=2),
+                out=w_grouped[key][:, half, :].rearrange("p (e b i) j -> p e b j i", e=2, i=4),
+                in_=w_rows[key][:, :, half].rearrange("p j (b i e) -> p e b j i", i=4, e=2),
             )
 
         def regroup_v(name, gh, g, u=0):

@@ -521,8 +521,8 @@ def tile_dynamicattention4_pa_kernel(tc, q, src, trg, Ws, b_s, Wt, b_t, out):
                 if unit[2] == last:
                     scale_at.setdefault(at + 1, []).append((unit, i))
 
-        steps = range(2, len(units))
-        due = {n: range((n - 2) * len(blocks) // len(steps), (n - 1) * len(blocks) // len(steps)) for n in steps}
+        steps = range(3, len(units))
+        due = {n: range((n - 3) * len(blocks) // len(steps), (n - 2) * len(blocks) // len(steps)) for n in steps}
         for n in steps:
             for m in due[n]:
                 if m % BLOCKS == BLOCKS - 1:
@@ -531,23 +531,21 @@ def tile_dynamicattention4_pa_kernel(tc, q, src, trg, Ws, b_s, Wt, b_t, out):
             plan(units[n], n + 2, 5 if n == 1 else n + 2)
 
         late_q = {
-            4: [(B_PE, 0, "acc11")],
-            5: [(B_PE, 1, "acc10"), (2, 0, "acc11")],
-            6: [(2, 1, "acc11")],
+            5: [(B_PE, 0, "acc11")],
+            6: [(B_PE, 1, "acc10"), (2, 0, "acc11")],
+            7: [(2, 1, "acc11")],
             11: [(3, 0, "acc10")],
             12: [(3, 1, "acc11")],
         }
         for n in range(2, final + 1):
-            if n == 4:
-                project(2, 1, "acc10")
             for m in due.get(n, []):
                 take_block_tanh(m)
             if n < len(units):
                 add_keys(n)
-            if n == 3:
+            if n == 4:
                 keep_keys(2, 0)
                 keep_rows(1)
-            if n == 4:
+            if n == 5:
                 keep_keys(2, 1)
             for unit, i in scale_at.get(n, []):
                 scale_scores(mul_v, unit, i)
@@ -556,8 +554,8 @@ def tile_dynamicattention4_pa_kernel(tc, q, src, trg, Ws, b_s, Wt, b_t, out):
                 quantise(unit)
             if n == 2:
                 quantise_q(0)
-            if n in (6, 8, 14):
-                quantise_q({6: B_PE, 8: 2, 14: 3}[n])
+            if n in (7, 9, 14):
+                quantise_q({7: B_PE, 9: 2, 14: 3}[n])
             for b, i, tag in late_q.get(n, []):
                 turn_q(b, i, psum_acc.tile([P, PASSES * 2, P], F32, name=tag))
             if n < final:
@@ -567,6 +565,8 @@ def tile_dynamicattention4_pa_kernel(tc, q, src, trg, Ws, b_s, Wt, b_t, out):
                 group_q(nc.scalar.copy, b, i)
             for unit, i in multiply_at.get(n, []):
                 multiply(unit, i)
+            if n == 4:
+                project(2, 1, "acc10")
             for m in due.get(n, []):
                 if m + 2 < len(blocks):
                     add_block(m + 2)

from contextlib import ExitStack

import concourse.mybir as mybir
from concourse.masks import make_identity

F32 = mybir.dt.float32
BF16 = mybir.dt.bfloat16
U32 = mybir.dt.uint32
U8 = mybir.dt.uint8
I32 = mybir.dt.int32
FP8X4 = mybir.dt.float8_e4m3fn_x4
ADD = mybir.AluOpType.add
TANH = mybir.ActivationFunctionType.Tanh

B, L, S, T, F, H = 4, 256, 32, 64, 1024, 1024
P = 128
PACK = 4
K_PASS = P * PACK
PASSES = F // K_PASS
T_CHUNK = 16
N_COLS = T_CHUNK * S
T_GPSIMD = 6
T_VECTOR = T_CHUNK - T_GPSIMD
B_PE = 1
BLOCK_T = 4
BLOCK_COLS = BLOCK_T * S
BLOCKS = T_CHUNK // BLOCK_T
RING = 5
L_TILES = L // P
SRC_TILES = B * S // P
TOKEN_TILES = SRC_TILES + B * T // P

FLOPS = 2 * (B * S + B * T) * F * H + 2 * B * L * T * S * H


def turn_rows(nc, bank, ident, rows):
    words = rows.bitcast(F32)
    for gu in range(PASSES * 2):
        nc.tensor.transpose(bank[:, gu, :], words[:, gu * P : (gu + 1) * P], ident)


def group_rows(copy, bank, grouped):
    copy(out=grouped.bitcast(F32), in_=bank[:].rearrange("p (g u) r -> p g r u", u=2))


def tile_dynamicattention4_pa_kernel(tc, q, src, trg, Ws, b_s, Wt, b_t, out):
    nc = tc.nc
    with ExitStack() as ctx:
        keep = ctx.enter_context(tc.tile_pool(name="keep", bufs=1))
        stage = ctx.enter_context(tc.tile_pool(name="stage", bufs=6))
        work = ctx.enter_context(tc.tile_pool(name="work", bufs=3))
        ring = ctx.enter_context(tc.tile_pool(name="ring", bufs=1))
        psum_turn = ctx.enter_context(tc.psum_pool(name="psum_turn", bufs=2))
        psum_src = ctx.enter_context(tc.psum_pool(name="psum_src", bufs=1))
        psum_acc = ctx.enter_context(tc.psum_pool(name="psum_acc", bufs=1))
        ctx.enter_context(tc.manual_schedule())

        ident = keep.tile([P, P], F32)
        nc.vector.memset(ident[:], 0.0)
        make_identity(nc, ident[:], nomemset=True)

        bias_rows = keep.tile([P, 2 * P], BF16)
        nc.vector.memset(bias_rows[:], 0.0)
        bias_row_count = H // (2 * P)
        nc.gpsimd.dma_start(
            out=bias_rows[0:bias_row_count, :], in_=b_s.rearrange("(r c) -> r c", c=2 * P)
        )
        nc.gpsimd.dma_start(
            out=bias_rows[bias_row_count : 2 * bias_row_count, :],
            in_=b_t.rearrange("(r c) -> r c", c=2 * P),
        )

        bias_flat = keep.tile([P, H], BF16)
        nc.gpsimd.memset(bias_flat[:], 0.0)
        nc.gpsimd.dma_start(out=bias_flat[0:1, :], in_=b_s.rearrange("(r c) -> r c", r=1))
        nc.gpsimd.dma_start(out=bias_flat[1:2, :], in_=b_t.rearrange("(r c) -> r c", r=1))

        pick = keep.tile([P, T, S], F32)
        pick_s = keep.tile([P, S], F32)
        nc.vector.tensor_copy(out=pick_s[:], in_=ident[:, S : 2 * S])
        nc.vector.memset(pick_s[0:S, :], 1.0)
        nc.vector.tensor_tensor(
            out=pick[:],
            in0=pick_s[:].unsqueeze(1).to_broadcast([P, T, S]),
            in1=ident[:, 2 * S :].unsqueeze(2).to_broadcast([P, T, S]),
            op=ADD,
        )

        pe_codes = {}
        pe_scales = {}
        for name in ("s", "t"):
            pe_codes[name] = keep.tile([P, PASSES, P], U32, name="pe_codes_%s" % name, align_bytes=64)
            pe_scales[name] = keep.tile([P, PASSES, P], U8, name="pe_scales_%s" % name, align_bytes=64)
            nc.gpsimd.memset(pe_codes[name][:], 0)
            nc.gpsimd.memset(pe_scales[name][:].bitcast(U32), 0)

        weights = {"s": Ws, "t": Wt}
        w_rows = {}

        def load_weight_columns(name, gh):
            cols = slice(gh * K_PASS, (gh + 1) * K_PASS)
            for g in range(PASSES):
                rows = keep.tile([P, PACK, K_PASS], BF16, name="w_rows_%s%d%d" % (name, gh, g))
                for u in range(2):
                    first = g * K_PASS + u * 2 * P
                    nc.sync.dma_start(
                        out=rows[:, 2 * u : 2 * u + 2, :],
                        in_=weights[name][first : first + 2 * P, cols].rearrange(
                            "(p e) c -> p e c", e=2
                        ),
                    )
                w_rows[(name, gh, g)] = rows

        load_weight_columns("t", 0)
        tokens = [src.flatten_outer_dims()] + [
            trg.flatten_outer_dims()[i * P : (i + 1) * P, :] for i in range(TOKEN_TILES - SRC_TILES)
        ]
        token_rows = [
            keep.tile([P, F], BF16, name="token_rows%d" % i) for i in range(TOKEN_TILES)
        ]
        for i in range(TOKEN_TILES):
            nc.sync.dma_start(out=token_rows[i][:], in_=tokens[i])
        load_weight_columns("s", 0)
        load_weight_columns("t", 1)
        load_weight_columns("s", 1)
        q_rows = [keep.tile([P, L_TILES, H], BF16, name="q_rows%d" % b) for b in range(B)]
        for b in (0, B_PE, 2, 3):
            nc.sync.dma_start(out=q_rows[b][:], in_=q[b].rearrange("(i p) h -> p i h", p=P))

        w_codes = {}
        w_scales = {}
        for name in weights:
            for gh in range(PASSES):
                w_codes[(name, gh)] = keep.tile(
                    [P, PASSES, K_PASS], U32, name="w_codes_%s%d" % (name, gh), align_bytes=64
                )
                w_scales[(name, gh)] = keep.tile(
                    [P, PASSES, K_PASS], U8, name="w_scales_%s%d" % (name, gh), align_bytes=64
                )
        w_grouped = {}

        def regroup(copy, u, name, gh, g):
            key = (name, gh, g)
            if key not in w_grouped:
                w_grouped[key] = stage.tile(
                    [P, K_PASS, PACK], BF16, align_bytes=64, tag="grouped", name="w_grouped"
                )
            half = slice(u * 2 * P, (u + 1) * 2 * P)
            copy(
                out=w_grouped[key][:, half, :].rearrange("p (e b i) j -> p e b j i", e=2, i=4),
                in_=w_rows[key][:, :, half].rearrange("p j (b i e) -> p e b j i", i=4, e=2),
            )

        def regroup_v(name, gh, g, u=0):
            regroup(nc.vector.tensor_copy, u, name, gh, g)

        def regroup_d(name, gh, g, u=1):
            regroup(nc.scalar.copy, u, name, gh, g)

        def quantise_weight(name, gh, g):
            nc.vector.quantize_mx(
                out=w_codes[(name, gh)][:, g, :].bitcast(FP8X4),
                scales=w_scales[(name, gh)][:, g, :],
                in_=w_grouped[(name, gh, g)][:].rearrange("p c j -> p (c j)"),
            )

        token_codes = keep.tile([P, TOKEN_TILES, PASSES, P], U32, align_bytes=64)
        token_scales = keep.tile([P, TOKEN_TILES, PASSES, P], U8, align_bytes=64)
        token_grouped = keep.tile([P, TOKEN_TILES, PASSES, P, PACK], BF16, align_bytes=64)

        def turn_token(i):
            bank = psum_turn.tile([P, PASSES * 2, P], F32, tag="turned")
            turn_rows(nc, bank, ident[:], token_rows[i][:])
            group_rows(nc.scalar.copy, bank, token_grouped[:, i])

        def quantise_token(i):
            nc.vector.quantize_mx(
                out=token_codes[:, i].rearrange("p g r -> p (g r)").bitcast(FP8X4),
                scales=token_scales[:, i].rearrange("p g r -> p (g r)"),
                in_=token_grouped[:, i].rearrange("p g r j -> p (g r j)"),
            )

        def pick_pe_codes():
            for name, tile_index, cols in (
                ("s", 0, slice(S, 2 * S)),
                ("t", SRC_TILES, slice(2 * S, 2 * S + T)),
            ):
                nc.vector.tensor_copy(
                    out=pe_codes[name][:, :, cols].bitcast(I32),
                    in_=token_codes[:, tile_index, :, cols].bitcast(I32),
                )
                nc.vector.tensor_copy(
                    out=pe_scales[name][:, :, cols], in_=token_scales[:, tile_index, :, cols]
                )

        bias_sum = keep.tile([P, PASSES, PACK], F32)

        def turn_biases():
            bank = psum_turn.tile([P, PASSES * 2, P], F32, tag="turned")
            nc.tensor.transpose(bank[:, 0, :], bias_rows[:].bitcast(F32), ident[:])
            bias_cols = keep.tile([P, 2, PASSES * PACK], F32)
            nc.vector.tensor_copy(
                out=bias_cols[:].rearrange("p w c -> p (w c)"),
                in_=bank[:, 0, 0 : 2 * bias_row_count].bitcast(BF16),
            )
            nc.vector.tensor_tensor(
                out=bias_sum[:].rearrange("p g j -> p (g j)"),
                in0=bias_cols[:, 0, :],
                in1=bias_cols[:, 1, :],
                op=ADD,
            )

        s_keys = keep.tile([P, PASSES, B * S, PACK], F32)
        t_keys = keep.tile([P, PASSES, B * T, PACK], F32)
        s_banks = [
            psum_src.tile([P, PACK, P], F32, name="s_bank%d" % gh) for gh in range(PASSES)
        ]

        key_banks = {}

        def project(i, gh, tag=None):
            name = "s" if i < SRC_TILES else "t"
            if i < SRC_TILES:
                key_bank = s_banks[gh]
            else:
                if tag is None:
                    key_bank = psum_turn.tile([P, PACK, P], F32, tag="turned")
                else:
                    key_bank = psum_acc.tile([P, PACK, P], F32, tag=tag)
            key_banks[(i, gh)] = key_bank
            for j in range(PACK):
                cols = slice(j * P, (j + 1) * P)
                for g in range(PASSES):
                    nc.tensor.matmul_mx(
                        out=key_bank[:, j, :],
                        lhsT=w_codes[(name, gh)][:, g, cols].bitcast(FP8X4),
                        lhsT_scale=w_scales[(name, gh)][:, g, cols],
                        rhs=token_codes[:, i, g, :].bitcast(FP8X4),
                        rhs_scale=token_scales[:, i, g, :],
                        start=(g == 0),
                        stop=(g == PASSES - 1),
                    )

        def keep_keys(i, gh):
            by_row = key_banks[(i, gh)][:].rearrange("p j r -> p r j")
            if i < SRC_TILES:
                nc.scalar.copy(out=s_keys[:, gh, :, :], in_=by_row)
            else:
                rows = slice((i - SRC_TILES) * P, (i - SRC_TILES + 1) * P)
                nc.vector.tensor_tensor(
                    out=t_keys[:, gh, rows, :],
                    in0=by_row,
                    in1=bias_sum[:, gh, :].unsqueeze(1).to_broadcast([P, P, PACK]),
                    op=ADD,
                )

        pe_keys = keep.tile([P, PASSES, K_PASS], F32)
        row_banks = {}

        def project_rows(gh, tag=None):
            if tag is None:
                bank = psum_turn.tile([P, K_PASS], F32, tag="turned")
            else:
                bank = psum_acc.tile([P, K_PASS], F32, tag=tag)
            steps = [(name, g) for name in ("t", "s") for g in range(PASSES)]
            for name, g in steps:
                nc.tensor.matmul_mx(
                    out=bank[:],
                    lhsT=pe_codes[name][:, g, :].bitcast(FP8X4),
                    lhsT_scale=pe_scales[name][:, g, :],
                    rhs=w_codes[(name, gh)][:, g, :].bitcast(FP8X4),
                    rhs_scale=w_scales[(name, gh)][:, g, :],
                    start=((name, g) == steps[0]),
                    stop=((name, g) == steps[-1]),
                )
            row_banks[gh] = bank

        def keep_rows(gh):
            nc.vector.tensor_tensor(
                out=pe_keys[:, gh, :].rearrange("p (u e c) -> p u e c", u=2, e=2),
                in0=row_banks[gh][:].rearrange("p (u e c) -> p u e c", u=2, e=2),
                in1=bias_flat[:, gh * K_PASS : (gh + 1) * K_PASS].rearrange(
                    "p (u c e) -> p u e c", u=2, e=2
                ),
                op=ADD,
            )

        q_codes = keep.tile([P, B * L_TILES, PASSES, P], U32, align_bytes=64)
        q_scales = keep.tile([P, B * L_TILES, PASSES, P], U8, align_bytes=64)
        q_grouped = {}

        q_banks = {}

        def turn_q(b, i, bank=None):
            if bank is None:
                bank = psum_acc.tile([P, PASSES * 2, P], F32, tag="acc%d%d" % (b == B_PE, i))
            turn_rows(nc, bank, ident[:], q_rows[b][:, i, :])
            q_banks[(b, i)] = bank

        def group_q(copy, b, i):
            if i == 0:
                q_grouped[b] = stage.tile(
                    [P, L_TILES, PASSES, P, PACK],
                    BF16,
                    align_bytes=64,
                    tag="grouped",
                    name="q_grouped",
                )
            group_rows(copy, q_banks[(b, i)], q_grouped[b][:, i])

        def quantise_q(b):
            tiles = slice(b * L_TILES, (b + 1) * L_TILES)
            nc.vector.quantize_mx(
                out=q_codes[:, tiles].rearrange("p i g r -> p (i g r)").bitcast(FP8X4),
                scales=q_scales[:, tiles].rearrange("p i g r -> p (i g r)"),
                in_=q_grouped[b][:].rearrange("p i g r j -> p (i g r j)"),
            )

        pairs = [(c, gh) for c in range(T // T_CHUNK) for gh in range(PASSES)]
        units = [(b, c, gh) for b in range(B) if b != B_PE for c, gh in pairs]
        units.append((B_PE,) + pairs[-1])
        units[1], units[2] = units[2], units[1]
        pe_units = [(B_PE, c, gh) for c, gh in pairs[:-1]]
        key_sums = {}
        rels = {}
        accs = {}

        def add_keys(n, vector_alone=False):
            b, c, gh = units[n]
            src_rows = slice(b * S, (b + 1) * S)
            first_t = b * T + c * T_CHUNK
            sum_g = ring.tile([P, T_GPSIMD, S, PACK], F32, name="ring%d" % (2 * n % RING), align_bytes=64)
            sum_v = work.tile([P, T_VECTOR, S, PACK], F32)
            nc.vector.tensor_tensor(
                out=sum_v[:],
                in0=s_banks[gh][:, :, src_rows]
                .rearrange("p j s -> p s j")
                .unsqueeze(1)
                .to_broadcast([P, T_VECTOR, S, PACK]),
                in1=t_keys[:, gh, first_t : first_t + T_VECTOR, :]
                .unsqueeze(2)
                .to_broadcast([P, T_VECTOR, S, PACK]),
                op=ADD,
            )
            if vector_alone:
                other = nc.vector
                src_keys = s_banks[gh][:, :, src_rows].rearrange("p j s -> p s j")
            else:
                other = nc.gpsimd
                src_keys = s_keys[:, gh, src_rows, :]
            other.tensor_tensor(
                out=sum_g[:],
                in0=src_keys.unsqueeze(1).to_broadcast([P, T_GPSIMD, S, PACK]),
                in1=t_keys[:, gh, first_t + T_VECTOR : first_t + T_CHUNK, :]
                .unsqueeze(2)
                .to_broadcast([P, T_GPSIMD, S, PACK]),
                op=ADD,
            )
            key_sums[n] = (sum_v, sum_g)

        split = T_VECTOR * S

        def take_tanh(n, first, stop):
            sum_v, sum_g = key_sums[n]
            if units[n] not in rels:
                rels[units[n]] = ring.tile(
                    [P, N_COLS * PACK],
                    BF16,
                    name="ring%d" % ((2 * n + 1) % RING),
                    align_bytes=64,
                )
            sums, start = (sum_v, 0) if stop <= split else (sum_g, split)
            nc.scalar.activation(
                out=rels[units[n]][:, first * PACK : stop * PACK],
                in_=sums[:].rearrange("p t s j -> p (t s j)")[
                    :, (first - start) * PACK : (stop - start) * PACK
                ],
                func=TANH,
            )

        blocks = [(unit, k) for unit in pe_units for k in range(BLOCKS)]
        block_banks = {}

        def add_block(m):
            (b, c, gh), k = blocks[m]
            bank = psum_turn.tile([P, PACK, BLOCK_COLS], F32, tag="turned")
            first_t = c * T_CHUNK + k * BLOCK_T
            for j in range(PACK):
                nc.tensor.matmul(
                    out=bank[:, j, :],
                    lhsT=pe_keys[:, gh, j * P : (j + 1) * P],
                    rhs=pick[:, first_t : first_t + BLOCK_T, :].rearrange("p t s -> p (t s)"),
                    start=True,
                    stop=True,
                )
            block_banks[m] = bank

        def take_block_tanh(m):
            unit, k = blocks[m]
            if k == 0:
                rels[unit] = work.tile([P, N_COLS * PACK], BF16, align_bytes=64, name="rel_pe")
            cols = slice(k * BLOCK_COLS * PACK, (k + 1) * BLOCK_COLS * PACK)
            nc.scalar.activation(
                out=rels[unit][:, cols].rearrange("p (c j) -> p c j", j=PACK),
                in_=block_banks[m][:].rearrange("p j c -> p c j"),
                func=TANH,
            )

        codes = {}

        whole = slice(0, N_COLS)

        def quantise(unit, cols=whole):
            if unit not in codes:
                rel_codes = work.tile([P, N_COLS], U32, align_bytes=64, bufs=6)
                rel_scales = work.tile([P, N_COLS], U8, align_bytes=64, bufs=6)
                codes[unit] = (rel_codes, rel_scales)
            nc.vector.quantize_mx(
                out=codes[unit][0][:, cols].bitcast(FP8X4),
                scales=codes[unit][1][:, cols],
                in_=rels[unit][:, cols.start * PACK : cols.stop * PACK],
            )

        def multiply(unit, i, cols=whole):
            b, c, gh = unit
            rel_codes, rel_scales = codes[unit]
            if (b, c, i) not in accs:
                accs[(b, c, i)] = psum_acc.tile([P, N_COLS], F32, name="acc%d%d" % (b == B_PE, i))
            nc.tensor.matmul_mx(
                out=accs[(b, c, i)][:, cols],
                lhsT=q_codes[:, b * L_TILES + i, gh, :].bitcast(FP8X4),
                lhsT_scale=q_scales[:, b * L_TILES + i, gh, :],
                rhs=rel_codes[:, cols].bitcast(FP8X4),
                rhs_scale=rel_scales[:, cols],
                start=(gh == 0),
                stop=(gh == PASSES - 1),
            )

        scores = {}

        def scale_scores(mul, unit, i, cols=whole):
            b, c, gh = unit
            if (unit, i) not in scores:
                scores[(unit, i)] = work.tile([P, N_COLS], F32, bufs=6, name="scores")
            mul(scores[(unit, i)][:, cols], accs[(b, c, i)][:, cols], H ** -0.5)

        def store_scores(unit, i, cols=whole):
            b, c, gh = unit
            nc.sync.dma_start(
                out=out[b, i * P : (i + 1) * P].rearrange("p t s -> p (t s)")[
                    :, c * N_COLS + cols.start : c * N_COLS + cols.stop
                ],
                in_=scores[(unit, i)][:, cols],
            )

        for g in range(PASSES):
            regroup_d("t", 0, g)
            regroup_v("t", 0, g)
        for g in range(PASSES):
            quantise_weight("t", 0, g)
        for i in range(TOKEN_TILES):
            turn_token(i)
        for i in range(TOKEN_TILES):
            quantise_token(i)
        turn_biases()
        for g in range(PASSES):
            regroup_d("s", 0, g)
            regroup_v("s", 0, g)
        project(1, 0)
        for g in range(PASSES):
            quantise_weight("s", 0, g)
        project(0, 0)
        for g in range(PASSES):
            regroup_d("t", 1, g)
        regroup_d("t", 1, 0, 0)
        keep_keys(1, 0)
        add_keys(0, True)
        keep_keys(0, 0)
        regroup_v("t", 1, 1)
        pick_pe_codes()
        for g in range(PASSES):
            quantise_weight("t", 1, g)
        project(1, 1)
        project_rows(0, "acc10")
        for i in range(L_TILES):
            turn_q(0, i)
        add_keys(1)
        take_tanh(0, split, N_COLS)
        take_tanh(0, 0, split)
        for g in range(PASSES):
            regroup_d("s", 1, g)
            regroup_v("s", 1, g)
        for g in range(PASSES):
            quantise_weight("s", 1, g)
        project(0, 1)
        take_tanh(1, split, N_COLS)
        take_tanh(1, 0, split)
        keep_keys(1, 1)
        keep_rows(0)
        keep_keys(0, 1)
        for m in (0, 1):
            add_block(m)
        project_rows(1, "acc11")
        project(2, 0, "acc10")
        for i in range(L_TILES):
            group_q(nc.scalar.copy, 0, i)

        last = PASSES - 1
        mul_s = nc.scalar.mul
        mul_v = nc.vector.tensor_scalar_mul
        quantise_at = {}
        multiply_at = {}
        scale_at = {}
        final = len(units) - 1

        def plan(unit, ready, start):
            quantise_at.setdefault(ready, []).append(unit)
            for i in range(L_TILES):
                at = start + i
                multiply_at.setdefault(at, []).append((unit, i))
                if unit[2] == last:
                    scale_at.setdefault(at + 1, []).append((unit, i))

        steps = range(3, len(units))
        due = {n: range((n - 3) * len(blocks) // len(steps), (n - 2) * len(blocks) // len(steps)) for n in steps}
        for n in steps:
            for m in due[n]:
                if m % BLOCKS == BLOCKS - 1:
                    plan(pe_units[m // BLOCKS], n + 1, n + 1)
        for n in range(final):
            plan(units[n], n + 2, 5 if n == 1 else n + 2)

        late_q = {
            5: [(B_PE, 0, "acc11")],
            6: [(B_PE, 1, "acc10"), (2, 0, "acc11")],
            7: [(2, 1, "acc11")],
            11: [(3, 0, "acc10")],
            12: [(3, 1, "acc11")],
        }
        for n in range(2, final + 1):
            for m in due.get(n, []):
                take_block_tanh(m)
            if n < len(units):
                add_keys(n)
            if n == 4:
                keep_keys(2, 0)
                keep_rows(1)
            if n == 5:
                keep_keys(2, 1)
            for unit, i in scale_at.get(n, []):
                scale_scores(mul_v, unit, i)
                store_scores(unit, i)
            for unit in quantise_at.get(n, []):
                quantise(unit)
            if n == 2:
                quantise_q(0)
            if n in (7, 9, 14):
                quantise_q({7: B_PE, 9: 2, 14: 3}[n])
            for b, i, tag in late_q.get(n, []):
                turn_q(b, i, psum_acc.tile([P, PASSES * 2, P], F32, name=tag))
            if n < final:
                take_tanh(n, split, N_COLS)
                take_tanh(n, 0, split)
            for b, i, tag in late_q.get(n, []):
                group_q(nc.scalar.copy, b, i)
            for unit, i in multiply_at.get(n, []):
                multiply(unit, i)
            if n == 4:
                project(2, 1, "acc10")
            for m in due.get(n, []):
                if m + 2 < len(blocks):
                    add_block(m + 2)

        half, quarter = N_COLS // 2, N_COLS // 4
        take_tanh(final, split, N_COLS)
        take_tanh(final, half, split)
        take_tanh(final, 0, quarter)
        take_tanh(final, quarter, half)
        before, opener = units[final - 1], pe_units[-1]
        for unit, i in scale_at[final + 1]:
            scale_scores(mul_v, unit, i)
            store_scores(unit, i)
        quantise(opener)
        quantise(before)
        for unit, i in multiply_at[final + 1]:
            if unit != opener:
                multiply(unit, i)
        multiply(before, 1)
        for cols in (slice(half, N_COLS), slice(0, quarter), slice(quarter, half)):
            quantise(units[final], cols)
            for i in range(L_TILES):
                multiply(opener, i, cols)
                multiply(units[final], i, cols)
        for i, mul in enumerate((mul_s, mul_v)):
            scale_scores(mul, before, i)
            store_scores(before, i)
        for cols in (slice(half, N_COLS), slice(0, half)):
            for i, mul in enumerate((mul_s, mul_v)):
                scale_scores(mul, units[final], i, cols)
                store_scores(units[final], i, cols)
